import numpy as np
import ml_dtypes


def mxq(x, axis, fmt="e4m3"):
    dtype, down = {"e4m3": (ml_dtypes.float8_e4m3fn, 7), "e5m2": (ml_dtypes.float8_e5m2, 14)}[fmt]
    v = np.moveaxis(np.asarray(x, np.float32).astype(ml_dtypes.bfloat16).astype(np.float64), axis, -1)
    blocks = v.reshape(v.shape[:-1] + (-1, 32))
    amax = np.abs(blocks).max(-1, keepdims=True)
    byte = np.maximum(np.where(amax > 0, np.frexp(amax)[1] - 1 + 127, 0) - down, 1)
    scale = np.exp2(byte - 127.0)
    codes = (blocks / scale).astype(np.float32).astype(dtype).astype(np.float64)
    return np.moveaxis((codes * scale).reshape(v.shape), -1, axis)


BF16 = ml_dtypes.bfloat16


def bf(x):
    return np.asarray(x, np.float32).astype(BF16)


def f64(x):
    return np.asarray(x).astype(np.float64)


B, I, O, G, P = 1024, 512, 512, 5, 3
GRID_RANGE = (-1.0, 1.0)
L = G + P


def make_grid():
    h = (GRID_RANGE[1] - GRID_RANGE[0]) / G
    n = G + 2 * P + 1
    return np.linspace(GRID_RANGE[0] - P * h, GRID_RANGE[1] + P * h, n)


def b_spline(x, grid, k):
    x = x[..., None]
    g = grid[None, None, :]
    basis = ((x >= g[..., :-1]) & (x < g[..., 1:])).astype(np.float64)
    for p in range(1, k + 1):
        left_denom = g[..., p:-1] - g[..., :-(p + 1)]
        right_denom = g[..., p + 1:] - g[..., 1:-p]
        left_denom = np.where(left_denom > 0, left_denom, np.ones_like(left_denom))
        right_denom = np.where(right_denom > 0, right_denom, np.ones_like(right_denom))
        left = (x - g[..., :-(p + 1)]) / left_denom * basis[..., :-1]
        right = (g[..., p + 1:] - x) / right_denom * basis[..., 1:]
        basis = left + right
    return basis


def setup_inputs():
    x = np.random.uniform(-1.0, 1.0, (B, I))
    base_weight = np.random.uniform(-1.0, 1.0, (O, I)) * 3.0 / np.sqrt(I)
    spline_weight = np.random.standard_normal((O, I, L)) * 1.5 / np.sqrt(I)
    g = np.random.standard_normal((B, O)) * np.exp2(np.random.randint(-12, 1, (B, 1)))
    return {"x": bf(x), "base_weight": bf(base_weight), "spline_weight": bf(spline_weight), "grad_out": bf(g)}


def reference(x, base_weight, spline_weight, grad_out):
    basis = b_spline(f64(x), make_grid(), P).reshape(B, I * L)
    gw = mxq(f64(grad_out), 0, "e5m2").T @ mxq(basis, 0, "e4m3")
    return gw.reshape(O, I, L)

@@ -1,0 +1,164 @@
+import math
+from contextlib import ExitStack
+
+import concourse.mybir as mybir
+
+FLOPS = 2 * 1024 * 512 * 4096
+BYTES = 2 * 1024 * 512 * 2 + 512 * 4096 * 4
+
+BF16 = mybir.dt.bfloat16
+F32 = mybir.dt.float32
+U32 = mybir.dt.uint32
+U8 = mybir.dt.uint8
+E4 = mybir.dt.float8_e4m3fn_x4
+E5 = mybir.dt.float8_e5m2_x4
+ACT = mybir.ActivationFunctionType
+ALU = mybir.AluOpType
+
+P = 128
+PASSES = 2
+PACK = 4
+FEAT = 512
+OUTS = 512
+SPL = 8
+IC = 64
+NCH = FEAT // IC
+N = PASSES * IC * PACK
+OT = OUTS // P
+
+K6 = 1.0 / math.sqrt(6.0)
+SX = math.sqrt(2.5 ** 3 / 6.0)
+TWO3 = 2.0 / 3.0
+
+
+def tile_kanlayer_kernel(tc, x, base_weight, spline_weight, grad_out, out):
+    nc = tc.nc
+    x_v = x.rearrange("(c p j) i -> p c j i", c=PASSES, p=P, j=PACK)
+    g_v = grad_out.rearrange("(c p j) o -> p c j o", c=PASSES, p=P, j=PACK)
+    out_v = out.rearrange("(t p) i l -> p t (i l)", p=P)
+
+    with ExitStack() as ctx:
+        keep = ctx.enter_context(tc.tile_pool(name="keep", bufs=1))
+        tmp = ctx.enter_context(tc.tile_pool(name="tmp", bufs=2))
+        stage = ctx.enter_context(tc.tile_pool(name="stage", bufs=3))
+        psum = ctx.enter_context(tc.psum_pool(name="psum", bufs=8))
+
+        x_raw = keep.tile([P, PASSES, PACK, FEAT], BF16)
+        g_raw = keep.tile([P, PASSES, PACK, OUTS], BF16)
+        for c in range(PASSES):
+            nc.sync.dma_start(out=x_raw[:, c], in_=x_v[:, c])
+        for c in range(PASSES):
+            nc.sync.dma_start(out=g_raw[:, c], in_=g_v[:, c])
+
+        g_grp = keep.tile([P, PASSES, OUTS, PACK], BF16, align_bytes=64)
+        g_codes = keep.tile([P, PASSES, OUTS], U32, align_bytes=64)
+        g_scales = keep.tile([P, PASSES, OUTS], U8, align_bytes=64)
+        for c in range(PASSES):
+            nc.scalar.copy(out=g_grp[:, c], in_=g_raw[:, c].rearrange("p j o -> p o j"))
+        nc.vector.quantize_mx(
+            out=g_codes[:].rearrange("p c o -> p (c o)").bitcast(E5),
+            scales=g_scales[:].rearrange("p c o -> p (c o)"),
+            in_=g_grp[:].rearrange("p c o j -> p (c o j)"),
+        )
+
+        for q in range(NCH):
+            feats = slice(q * IC, (q + 1) * IC)
+            xg = tmp.tile([P, PASSES, IC, PACK], BF16)
+            nc.vector.tensor_copy(
+                out=xg[:].rearrange("p c (a b) j -> p c a j b", b=4),
+                in_=x_raw[:, :, :, feats].rearrange("p c j (a b) -> p c a j b", b=4),
+            )
+            xf = xg[:].rearrange("p c i j -> p (c i j)")
+
+            dist = tmp.tile([P, 2, N], F32)
+            nc.scalar.activation(out=dist[:, 0, :], in_=xf, func=ACT.Abs, bias=-0.5, scale=2.5)
+            nc.scalar.activation(out=dist[:, 1, :], in_=xf, func=ACT.Abs, bias=0.5, scale=2.5)
+            dist_sq = tmp.tile([P, 2, N], F32)
+            nc.scalar.activation(out=dist_sq[:], in_=dist[:], func=ACT.Square, bias=-2.0 * K6, scale=K6)
+            x_sq = tmp.tile([P, 2, N], F32)
+            nc.scalar.activation(out=x_sq[:, 0, :], in_=xf, func=ACT.Square, bias=0.2 * SX, scale=SX)
+            nc.scalar.activation(out=x_sq[:, 1, :], in_=xf, func=ACT.Square, bias=-0.2 * SX, scale=SX)
+            fold = tmp.tile([P, N], F32)
+            nc.scalar.activation(out=fold[:], in_=dist[:, 0, :], func=ACT.Abs, bias=-1.0, scale=1.0)
+            half_p = tmp.tile([P, N], F32)
+            nc.scalar.activation(out=half_p[:], in_=fold[:], func=ACT.Abs, bias=-0.5, scale=0.5)
+            p_sq = tmp.tile([P, 2, N], F32)
+            nc.scalar.activation(out=p_sq[:, 0, :], in_=fold[:], func=ACT.Square, bias=-1.0, scale=1.0)
+            nc.scalar.activation(out=p_sq[:, 1, :], in_=half_p[:], func=ACT.Square, bias=1.0, scale=-2.0)
+
+            cubes = tmp.tile([P, 4, N], BF16)
+            nc.vector.scalar_tensor_tensor(
+                out=cubes[:, 0:4:3, :], in0=dist[:], scalar=2.0, in1=dist_sq[:],
+                op0=ALU.subtract, op1=ALU.mult,
+            )
+            nc.vector.scalar_tensor_tensor(
+                out=cubes[:, 1, :], in0=xf, scalar=0.2, in1=x_sq[:, 0, :], op0=ALU.add, op1=ALU.mult,
+            )
+            nc.vector.scalar_tensor_tensor(
+                out=cubes[:, 2, :], in0=xf, scalar=0.2, in1=x_sq[:, 1, :], op0=ALU.subtract, op1=ALU.mult,
+            )
+            hump_raw = tmp.tile([P, 2, N], F32)
+            nc.vector.scalar_tensor_tensor(
+                out=hump_raw[:, 0, :], in0=half_p[:], scalar=1.0, in1=p_sq[:, 0, :],
+                op0=ALU.subtract, op1=ALU.mult,
+            )
+            nc.vector.scalar_tensor_tensor(
+                out=hump_raw[:, 1, :], in0=half_p[:], scalar=0.5, in1=p_sq[:, 1, :],
+                op0=ALU.add, op1=ALU.mult,
+            )
+            hump = tmp.tile([P, 2, N], BF16)
+            nc.vector.tensor_scalar(
+                out=hump[:, 0, :], in0=hump_raw[:, 0, :], scalar1=TWO3, scalar2=None, op0=ALU.add,
+            )
+            nc.vector.tensor_scalar(
+                out=hump[:, 1, :], in0=hump_raw[:, 1, :], scalar1=-1.0, scalar2=TWO3,
+                op0=ALU.mult, op1=ALU.add,
+            )
+
+            parts = tmp.tile([P, SPL, N], BF16)
+            nc.vector.tensor_scalar(
+                out=parts[:, 0, :], in0=cubes[:, 0, :], scalar1=0.0, scalar2=None, op0=ALU.max,
+            )
+            nc.vector.tensor_scalar(
+                out=parts[:, 1:4, :], in0=cubes[:, 1:4, :], scalar1=-1.0, scalar2=0.0,
+                op0=ALU.mult, op1=ALU.max,
+            )
+            nc.vector.tensor_scalar(
+                out=parts[:, 4, :], in0=cubes[:, 0, :], scalar1=-1.0, scalar2=0.0,
+                op0=ALU.mult, op1=ALU.max,
+            )
+            nc.vector.tensor_scalar(
+                out=parts[:, 5:8, :], in0=cubes[:, 1:4, :], scalar1=0.0, scalar2=None, op0=ALU.max,
+            )
+
+            basis = tmp.tile([P, PASSES, IC, SPL, PACK], BF16, align_bytes=64)
+            for h in range(SPL // 2):
+                nc.vector.tensor_tensor(
+                    out=basis[:, :, :, 2 * h : 2 * h + 2, :].rearrange("p c i l j -> p (c i) l j"),
+                    in0=parts[:, 2 * h : 2 * h + 2, :].rearrange("p l (n j) -> p n l j", j=PACK),
+                    in1=hump[:].rearrange("p r (n j) -> p n r j", j=PACK),
+                    op=ALU.min,
+                )
+            b_codes = tmp.tile([P, PASSES, IC * SPL], U32, align_bytes=64)
+            b_scales = tmp.tile([P, PASSES, IC * SPL], U8, align_bytes=64)
+            nc.vector.quantize_mx(
+                out=b_codes[:].rearrange("p c w -> p (c w)").bitcast(E4),
+                scales=b_scales[:].rearrange("p c w -> p (c w)"),
+                in_=basis[:].rearrange("p c i l j -> p (c i l j)"),
+            )
+
+            res = stage.tile([P, OT, IC * SPL], F32)
+            for t in range(OT):
+                acc = psum.tile([P, IC * SPL], F32)
+                for c in range(PASSES):
+                    nc.tensor.matmul_mx(
+                        out=acc[:],
+                        lhsT=g_codes[:, c, t * P : (t + 1) * P].bitcast(E5),
+                        lhsT_scale=g_scales[:, c, t * P : (t + 1) * P],
+                        rhs=b_codes[:, c, :].bitcast(E4),
+                        rhs_scale=b_scales[:, c, :],
+                        start=(c == 0),
+                        stop=(c == PASSES - 1),
+                    )
+                nc.scalar.copy(out=res[:, t, :], in_=acc[:])
+            nc.sync.dma_start(out=out_v[:, :, q * IC * SPL : (q + 1) * IC * SPL], in_=res[:])

@@ -24,11 +24,14 @@ SPL = 8
 IC = 64
 NCH = FEAT // IC
 N = PASSES * IC * PACK
+W = IC * SPL
 OT = OUTS // P
 
 K6 = 1.0 / math.sqrt(6.0)
 SX = math.sqrt(2.5 ** 3 / 6.0)
 TWO3 = 2.0 / 3.0
+
+HEAD = 128
 
 
 def tile_kanlayer_kernel(tc, x, base_weight, spline_weight, grad_out, out):
@@ -38,66 +41,89 @@ def tile_kanlayer_kernel(tc, x, base_weight, spline_weight, grad_out, out):
     out_v = out.rearrange("(t p) i l -> p t (i l)", p=P)
 
     with ExitStack() as ctx:
+        ctx.enter_context(tc.manual_schedule())
         keep = ctx.enter_context(tc.tile_pool(name="keep", bufs=1))
-        tmp = ctx.enter_context(tc.tile_pool(name="tmp", bufs=2))
+        xgp = ctx.enter_context(tc.tile_pool(name="xgp", bufs=4))
+        apool = ctx.enter_context(tc.tile_pool(name="apool", bufs=3))
+        vpool = ctx.enter_context(tc.tile_pool(name="vpool", bufs=2))
+        cpool = ctx.enter_context(tc.tile_pool(name="cpool", bufs=3))
         stage = ctx.enter_context(tc.tile_pool(name="stage", bufs=3))
         psum = ctx.enter_context(tc.psum_pool(name="psum", bufs=8))
 
-        x_raw = keep.tile([P, PASSES, PACK, FEAT], BF16)
+        x_head = keep.tile([P, PASSES, PACK, HEAD], BF16)
+        x_rest = keep.tile([P, PASSES, PACK, FEAT - HEAD], BF16)
         g_raw = keep.tile([P, PASSES, PACK, OUTS], BF16)
         for c in range(PASSES):
-            nc.sync.dma_start(out=x_raw[:, c], in_=x_v[:, c])
+            nc.sync.dma_start(out=x_head[:, c], in_=x_v[:, c, :, 0:HEAD])
+        for c in range(PASSES):
+            nc.sync.dma_start(out=x_rest[:, c], in_=x_v[:, c, :, HEAD:FEAT])
         for c in range(PASSES):
             nc.sync.dma_start(out=g_raw[:, c], in_=g_v[:, c])
 
         g_grp = keep.tile([P, PASSES, OUTS, PACK], BF16, align_bytes=64)
         g_codes = keep.tile([P, PASSES, OUTS], U32, align_bytes=64)
         g_scales = keep.tile([P, PASSES, OUTS], U8, align_bytes=64)
-        for c in range(PASSES):
-            nc.scalar.copy(out=g_grp[:, c], in_=g_raw[:, c].rearrange("p j o -> p o j"))
-        nc.vector.quantize_mx(
-            out=g_codes[:].rearrange("p c o -> p (c o)").bitcast(E5),
-            scales=g_scales[:].rearrange("p c o -> p (c o)"),
-            in_=g_grp[:].rearrange("p c o j -> p (c o j)"),
-        )
 
-        for q in range(NCH):
-            feats = slice(q * IC, (q + 1) * IC)
-            xg = tmp.tile([P, PASSES, IC, PACK], BF16)
-            nc.vector.tensor_copy(
-                out=xg[:].rearrange("p c (a b) j -> p c a j b", b=4),
-                in_=x_raw[:, :, :, feats].rearrange("p c j (a b) -> p c a j b", b=4),
-            )
-            xf = xg[:].rearrange("p c i j -> p (c i j)")
+        live = {}
 
-            dist = tmp.tile([P, 2, N], F32)
-            nc.scalar.activation(out=dist[:, 0, :], in_=xf, func=ACT.Abs, bias=-0.5, scale=2.5)
-            nc.scalar.activation(out=dist[:, 1, :], in_=xf, func=ACT.Abs, bias=0.5, scale=2.5)
-            dist_sq = tmp.tile([P, 2, N], F32)
-            nc.scalar.activation(out=dist_sq[:], in_=dist[:], func=ACT.Square, bias=-2.0 * K6, scale=K6)
-            x_sq = tmp.tile([P, 2, N], F32)
+        def regroup(q):
+            if q * IC < HEAD:
+                src = x_head[:, :, :, q * IC : (q + 1) * IC]
+            else:
+                src = x_rest[:, :, :, q * IC - HEAD : (q + 1) * IC - HEAD]
+            xg = xgp.tile([P, PASSES, IC, PACK], BF16, name="xg")
+            if q < 2:
+                nc.vector.tensor_copy(
+                    out=xg[:].rearrange("p c (a b) j -> p c a j b", b=4),
+                    in_=src.rearrange("p c j (a b) -> p c a j b", b=4),
+                )
+            else:
+                nc.scalar.copy(out=xg[:], in_=src.rearrange("p c j i -> p c i j"))
+            live[("xf", q)] = xg[:].rearrange("p c i j -> p (c i j)")
+
+        def scalar_part(q):
+            xf = live[("xf", q)]
+            x_sq = apool.tile([P, 2, N], F32, name="x_sq")
             nc.scalar.activation(out=x_sq[:, 0, :], in_=xf, func=ACT.Square, bias=0.2 * SX, scale=SX)
             nc.scalar.activation(out=x_sq[:, 1, :], in_=xf, func=ACT.Square, bias=-0.2 * SX, scale=SX)
-            fold = tmp.tile([P, N], F32)
+            dist = apool.tile([P, 2, N], F32, name="dist")
+            nc.scalar.activation(out=dist[:, 0, :], in_=xf, func=ACT.Abs, bias=-0.5, scale=2.5)
+            fold = apool.tile([P, N], F32, name="fold")
             nc.scalar.activation(out=fold[:], in_=dist[:, 0, :], func=ACT.Abs, bias=-1.0, scale=1.0)
-            half_p = tmp.tile([P, N], F32)
+            half_p = apool.tile([P, N], F32, name="half_p")
             nc.scalar.activation(out=half_p[:], in_=fold[:], func=ACT.Abs, bias=-0.5, scale=0.5)
-            p_sq = tmp.tile([P, 2, N], F32)
+            p_sq = apool.tile([P, 2, N], F32, name="p_sq")
             nc.scalar.activation(out=p_sq[:, 0, :], in_=fold[:], func=ACT.Square, bias=-1.0, scale=1.0)
             nc.scalar.activation(out=p_sq[:, 1, :], in_=half_p[:], func=ACT.Square, bias=1.0, scale=-2.0)
+            nc.scalar.activation(out=dist[:, 1, :], in_=xf, func=ACT.Abs, bias=0.5, scale=2.5)
+            dist_sq = apool.tile([P, 2, N], F32, name="dist_sq")
+            nc.scalar.activation(out=dist_sq[:], in_=dist[:], func=ACT.Square, bias=-2.0 * K6, scale=K6)
+            live[("act", q)] = (x_sq, dist, dist_sq, half_p, p_sq)
 
-            cubes = tmp.tile([P, 4, N], BF16)
-            nc.vector.scalar_tensor_tensor(
-                out=cubes[:, 0:4:3, :], in0=dist[:], scalar=2.0, in1=dist_sq[:],
-                op0=ALU.subtract, op1=ALU.mult,
+        def regroup_g(c):
+            nc.vector.tensor_copy(
+                out=g_grp[:, c].rearrange("p (a b) j -> p a j b", b=4),
+                in_=g_raw[:, c].rearrange("p j (a b) -> p a j b", b=4),
             )
+
+        def vector_first(q):
+            xf = live[("xf", q)]
+            x_sq = live[("act", q)][0]
+            cubes = vpool.tile([P, 4, N], BF16, name="cubes")
             nc.vector.scalar_tensor_tensor(
                 out=cubes[:, 1, :], in0=xf, scalar=0.2, in1=x_sq[:, 0, :], op0=ALU.add, op1=ALU.mult,
             )
             nc.vector.scalar_tensor_tensor(
                 out=cubes[:, 2, :], in0=xf, scalar=0.2, in1=x_sq[:, 1, :], op0=ALU.subtract, op1=ALU.mult,
             )
-            hump_raw = tmp.tile([P, 2, N], F32)
+            live[("cubes", q)] = cubes
+
+        def vector_rest(q):
+            x_sq, dist, dist_sq, half_p, p_sq = live[("act", q)]
+            cubes = live[("cubes", q)]
+            if q == 0:
+                regroup_g(0)
+            hump_raw = vpool.tile([P, 2, N], F32, name="hump_raw")
             nc.vector.scalar_tensor_tensor(
                 out=hump_raw[:, 0, :], in0=half_p[:], scalar=1.0, in1=p_sq[:, 0, :],
                 op0=ALU.subtract, op1=ALU.mult,
@@ -106,7 +132,14 @@ def tile_kanlayer_kernel(tc, x, base_weight, spline_weight, grad_out, out):
                 out=hump_raw[:, 1, :], in0=half_p[:], scalar=0.5, in1=p_sq[:, 1, :],
                 op0=ALU.add, op1=ALU.mult,
             )
-            hump = tmp.tile([P, 2, N], BF16)
+            if q == 0:
+                regroup_g(1)
+            nc.vector.scalar_tensor_tensor(
+                out=cubes[:, 0:4:3, :], in0=dist[:], scalar=2.0, in1=dist_sq[:],
+                op0=ALU.subtract, op1=ALU.mult,
+            )
+            parts = vpool.tile([P, SPL, N], BF16, name="parts")
+            hump = vpool.tile([P, 2, N], BF16, name="hump")
             nc.vector.tensor_scalar(
                 out=hump[:, 0, :], in0=hump_raw[:, 0, :], scalar1=TWO3, scalar2=None, op0=ALU.add,
             )
@@ -114,45 +147,56 @@ def tile_kanlayer_kernel(tc, x, base_weight, spline_weight, grad_out, out):
                 out=hump[:, 1, :], in0=hump_raw[:, 1, :], scalar1=-1.0, scalar2=TWO3,
                 op0=ALU.mult, op1=ALU.add,
             )
-
-            parts = tmp.tile([P, SPL, N], BF16)
-            nc.vector.tensor_scalar(
-                out=parts[:, 0, :], in0=cubes[:, 0, :], scalar1=0.0, scalar2=None, op0=ALU.max,
-            )
             nc.vector.tensor_scalar(
                 out=parts[:, 1:4, :], in0=cubes[:, 1:4, :], scalar1=-1.0, scalar2=0.0,
                 op0=ALU.mult, op1=ALU.max,
             )
             nc.vector.tensor_scalar(
+                out=parts[:, 5:8, :], in0=cubes[:, 1:4, :], scalar1=0.0, scalar2=None, op0=ALU.max,
+            )
+            nc.vector.tensor_scalar(
+                out=parts[:, 0, :], in0=cubes[:, 0, :], scalar1=0.0, scalar2=None, op0=ALU.max,
+            )
+            nc.vector.tensor_scalar(
                 out=parts[:, 4, :], in0=cubes[:, 0, :], scalar1=-1.0, scalar2=0.0,
                 op0=ALU.mult, op1=ALU.max,
             )
-            nc.vector.tensor_scalar(
-                out=parts[:, 5:8, :], in0=cubes[:, 1:4, :], scalar1=0.0, scalar2=None, op0=ALU.max,
-            )
-
-            basis = tmp.tile([P, PASSES, IC, SPL, PACK], BF16, align_bytes=64)
-            for h in range(SPL // 2):
+            basis = vpool.tile([P, PASSES, IC, SPL, PACK], BF16, name="basis", align_bytes=64)
+            for h in (1, 3, 0, 2):
                 nc.vector.tensor_tensor(
                     out=basis[:, :, :, 2 * h : 2 * h + 2, :].rearrange("p c i l j -> p (c i) l j"),
                     in0=parts[:, 2 * h : 2 * h + 2, :].rearrange("p l (n j) -> p n l j", j=PACK),
                     in1=hump[:].rearrange("p r (n j) -> p n r j", j=PACK),
                     op=ALU.min,
                 )
-            b_codes = tmp.tile([P, PASSES, IC * SPL], U32, align_bytes=64)
-            b_scales = tmp.tile([P, PASSES, IC * SPL], U8, align_bytes=64)
-            nc.vector.quantize_mx(
-                out=b_codes[:].rearrange("p c w -> p (c w)").bitcast(E4),
-                scales=b_scales[:].rearrange("p c w -> p (c w)"),
-                in_=basis[:].rearrange("p c i l j -> p (c i l j)"),
-            )
+            live[("basis", q)] = basis
 
-            res = stage.tile([P, OT, IC * SPL], F32)
-            for t in range(OT):
-                acc = psum.tile([P, IC * SPL], F32)
+        def quantise(q):
+            basis = live[("basis", q)]
+            b_codes = cpool.tile([P, PASSES, W], U32, name="b_codes", align_bytes=64)
+            b_scales = cpool.tile([P, PASSES, W], U8, name="b_scales", align_bytes=64)
+            if q == NCH - 1:
                 for c in range(PASSES):
+                    nc.vector.quantize_mx(
+                        out=b_codes[:, c, :].bitcast(E4),
+                        scales=b_scales[:, c, :],
+                        in_=basis[:, c].rearrange("p i l j -> p (i l j)"),
+                    )
+            else:
+                nc.vector.quantize_mx(
+                    out=b_codes[:].rearrange("p c w -> p (c w)").bitcast(E4),
+                    scales=b_scales[:].rearrange("p c w -> p (c w)"),
+                    in_=basis[:].rearrange("p c i l j -> p (c i l j)"),
+                )
+            live[("codes", q)] = (b_codes, b_scales)
+
+        def multiply(q):
+            b_codes, b_scales = live[("codes", q)]
+            banks = [psum.tile([P, W], F32, name="acc") for t in range(OT)]
+            for c in range(PASSES):
+                for t in range(OT):
                     nc.tensor.matmul_mx(
-                        out=acc[:],
+                        out=banks[t][:],
                         lhsT=g_codes[:, c, t * P : (t + 1) * P].bitcast(E5),
                         lhsT_scale=g_scales[:, c, t * P : (t + 1) * P],
                         rhs=b_codes[:, c, :].bitcast(E4),
@@ -160,5 +204,42 @@ def tile_kanlayer_kernel(tc, x, base_weight, spline_weight, grad_out, out):
                         start=(c == 0),
                         stop=(c == PASSES - 1),
                     )
-                nc.scalar.copy(out=res[:, t, :], in_=acc[:])
-            nc.sync.dma_start(out=out_v[:, :, q * IC * SPL : (q + 1) * IC * SPL], in_=res[:])
+            live[("banks", q)] = banks
+
+        def empty(q, last):
+            banks = live[("banks", q)]
+            res = stage.tile([P, OT, W], F32, name="res")
+            cols = slice(q * W, (q + 1) * W)
+            for t in range(OT):
+                if last and t % 2 == 1:
+                    nc.vector.tensor_copy(out=res[:, t, :], in_=banks[t][:])
+                else:
+                    nc.scalar.copy(out=res[:, t, :], in_=banks[t][:])
+                if last and t % 2 == 1:
+                    nc.sync.dma_start(out=out_v[:, t - 1 : t + 1, cols], in_=res[:, t - 1 : t + 1, :])
+            if not last:
+                nc.sync.dma_start(out=out_v[:, :, cols], in_=res[:])
+
+        regroup(0)
+        scalar_part(0)
+        regroup(1)
+        scalar_part(1)
+        regroup(2)
+        vector_first(0)
+        for q in range(NCH):
+            vector_rest(q)
+            if q + 1 < NCH:
+                vector_first(q + 1)
+            quantise(q)
+            if q == 0:
+                nc.vector.quantize_mx(
+                    out=g_codes[:].rearrange("p c o -> p (c o)").bitcast(E5),
+                    scales=g_scales[:].rearrange("p c o -> p (c o)"),
+                    in_=g_grp[:].rearrange("p c o j -> p (c o j)"),
+                )
+            multiply(q)
+            if q + 2 < NCH:
+                scalar_part(q + 2)
+            if q + 3 < NCH:
+                regroup(q + 3)
+            empty(q, q == NCH - 1)

@@ -21,17 +21,15 @@ PACK = 4
 FEAT = 512
 OUTS = 512
 SPL = 8
-IC = 64
-NCH = FEAT // IC
-N = PASSES * IC * PACK
-W = IC * SPL
+GRP = 64
+W = GRP * SPL
+SIZES = (64, 128, 128, 128, 64)
+ON_VECTOR = (0, 1, 2)
 OT = OUTS // P
 
 K6 = 1.0 / math.sqrt(6.0)
 SX = math.sqrt(2.5 ** 3 / 6.0)
 TWO3 = 2.0 / 3.0
-
-HEAD = 128
 
 
 def tile_kanlayer_kernel(tc, x, base_weight, spline_weight, grad_out, out):
@@ -39,24 +37,28 @@ def tile_kanlayer_kernel(tc, x, base_weight, spline_weight, grad_out, out):
     x_v = x.rearrange("(c p j) i -> p c j i", c=PASSES, p=P, j=PACK)
     g_v = grad_out.rearrange("(c p j) o -> p c j o", c=PASSES, p=P, j=PACK)
     out_v = out.rearrange("(t p) i l -> p t (i l)", p=P)
+    nch = len(SIZES)
+    starts = [sum(SIZES[:e]) for e in range(nch)]
+    head = SIZES[0]
 
     with ExitStack() as ctx:
         ctx.enter_context(tc.manual_schedule())
         keep = ctx.enter_context(tc.tile_pool(name="keep", bufs=1))
-        xgp = ctx.enter_context(tc.tile_pool(name="xgp", bufs=4))
-        apool = ctx.enter_context(tc.tile_pool(name="apool", bufs=3))
-        vpool = ctx.enter_context(tc.tile_pool(name="vpool", bufs=2))
-        cpool = ctx.enter_context(tc.tile_pool(name="cpool", bufs=3))
+        xgp = ctx.enter_context(tc.tile_pool(name="xgp", bufs=3))
+        apool = ctx.enter_context(tc.tile_pool(name="apool", bufs=2))
+        vone = ctx.enter_context(tc.tile_pool(name="vone", bufs=1))
+        vtwo = ctx.enter_context(tc.tile_pool(name="vtwo", bufs=2))
+        cpool = ctx.enter_context(tc.tile_pool(name="cpool", bufs=2))
         stage = ctx.enter_context(tc.tile_pool(name="stage", bufs=3))
         psum = ctx.enter_context(tc.psum_pool(name="psum", bufs=8))
 
-        x_head = keep.tile([P, PASSES, PACK, HEAD], BF16)
-        x_rest = keep.tile([P, PASSES, PACK, FEAT - HEAD], BF16)
-        g_raw = keep.tile([P, PASSES, PACK, OUTS], BF16)
+        x_head = keep.tile([P, PASSES, PACK, head], BF16)
+        x_rest = keep.tile([P, PASSES, PACK, FEAT - head], BF16)
+        g_raw = vone.tile([P, PASSES, PACK, OUTS], BF16, tag="parts")
         for c in range(PASSES):
-            nc.sync.dma_start(out=x_head[:, c], in_=x_v[:, c, :, 0:HEAD])
+            nc.sync.dma_start(out=x_head[:, c], in_=x_v[:, c, :, 0:head])
         for c in range(PASSES):
-            nc.sync.dma_start(out=x_rest[:, c], in_=x_v[:, c, :, HEAD:FEAT])
+            nc.sync.dma_start(out=x_rest[:, c], in_=x_v[:, c, :, head:FEAT])
         for c in range(PASSES):
             nc.sync.dma_start(out=g_raw[:, c], in_=g_v[:, c])
 
@@ -66,39 +68,41 @@ def tile_kanlayer_kernel(tc, x, base_weight, spline_weight, grad_out, out):
 
         live = {}
 
-        def regroup(q):
-            if q * IC < HEAD:
-                src = x_head[:, :, :, q * IC : (q + 1) * IC]
+        def regroup(e):
+            size = SIZES[e]
+            if e == 0:
+                src = x_head[:]
             else:
-                src = x_rest[:, :, :, q * IC - HEAD : (q + 1) * IC - HEAD]
-            xg = xgp.tile([P, PASSES, IC, PACK], BF16, name="xg")
-            if q < 2:
+                src = x_rest[:, :, :, starts[e] - head : starts[e] - head + size]
+            xg = xgp.tile([P, PASSES, size, PACK], BF16, name="xg")
+            if e in ON_VECTOR:
                 nc.vector.tensor_copy(
                     out=xg[:].rearrange("p c (a b) j -> p c a j b", b=4),
                     in_=src.rearrange("p c j (a b) -> p c a j b", b=4),
                 )
             else:
                 nc.scalar.copy(out=xg[:], in_=src.rearrange("p c j i -> p c i j"))
-            live[("xf", q)] = xg[:].rearrange("p c i j -> p (c i j)")
+            live[("xf", e)] = xg[:].rearrange("p c i j -> p (c i j)")
 
-        def scalar_part(q):
-            xf = live[("xf", q)]
-            x_sq = apool.tile([P, 2, N], F32, name="x_sq")
-            nc.scalar.activation(out=x_sq[:, 0, :], in_=xf, func=ACT.Square, bias=0.2 * SX, scale=SX)
-            nc.scalar.activation(out=x_sq[:, 1, :], in_=xf, func=ACT.Square, bias=-0.2 * SX, scale=SX)
-            dist = apool.tile([P, 2, N], F32, name="dist")
+        def scalar_part(e):
+            n = PASSES * SIZES[e] * PACK
+            xf = live[("xf", e)]
+            x_sq = apool.tile([P, 2, n], F32, name="x_sq")
+            dist = apool.tile([P, 2, n], F32, name="dist")
+            dist_sq = apool.tile([P, 2, n], F32, name="dist_sq")
+            fold = apool.tile([P, n], F32, name="fold")
+            half_p = apool.tile([P, n], F32, name="half_p")
+            p_sq = apool.tile([P, 2, n], F32, name="p_sq")
             nc.scalar.activation(out=dist[:, 0, :], in_=xf, func=ACT.Abs, bias=-0.5, scale=2.5)
-            fold = apool.tile([P, N], F32, name="fold")
+            nc.scalar.activation(out=x_sq[:, 0, :], in_=xf, func=ACT.Square, bias=0.2 * SX, scale=SX)
             nc.scalar.activation(out=fold[:], in_=dist[:, 0, :], func=ACT.Abs, bias=-1.0, scale=1.0)
-            half_p = apool.tile([P, N], F32, name="half_p")
+            nc.scalar.activation(out=x_sq[:, 1, :], in_=xf, func=ACT.Square, bias=-0.2 * SX, scale=SX)
             nc.scalar.activation(out=half_p[:], in_=fold[:], func=ACT.Abs, bias=-0.5, scale=0.5)
-            p_sq = apool.tile([P, 2, N], F32, name="p_sq")
+            nc.scalar.activation(out=dist[:, 1, :], in_=xf, func=ACT.Abs, bias=0.5, scale=2.5)
             nc.scalar.activation(out=p_sq[:, 0, :], in_=fold[:], func=ACT.Square, bias=-1.0, scale=1.0)
             nc.scalar.activation(out=p_sq[:, 1, :], in_=half_p[:], func=ACT.Square, bias=1.0, scale=-2.0)
-            nc.scalar.activation(out=dist[:, 1, :], in_=xf, func=ACT.Abs, bias=0.5, scale=2.5)
-            dist_sq = apool.tile([P, 2, N], F32, name="dist_sq")
             nc.scalar.activation(out=dist_sq[:], in_=dist[:], func=ACT.Square, bias=-2.0 * K6, scale=K6)
-            live[("act", q)] = (x_sq, dist, dist_sq, half_p, p_sq)
+            live[("act", e)] = (x_sq, dist, dist_sq, half_p, p_sq)
 
         def regroup_g(c):
             nc.vector.tensor_copy(
@@ -106,24 +110,27 @@ def tile_kanlayer_kernel(tc, x, base_weight, spline_weight, grad_out, out):
                 in_=g_raw[:, c].rearrange("p j (a b) -> p a j b", b=4),
             )
 
-        def vector_first(q):
-            xf = live[("xf", q)]
-            x_sq = live[("act", q)][0]
-            cubes = vpool.tile([P, 4, N], BF16, name="cubes")
+        def vector_first(e):
+            n = PASSES * SIZES[e] * PACK
+            xf = live[("xf", e)]
+            x_sq = live[("act", e)][0]
+            cubes = vtwo.tile([P, 4, n], BF16, name="cubes")
             nc.vector.scalar_tensor_tensor(
                 out=cubes[:, 1, :], in0=xf, scalar=0.2, in1=x_sq[:, 0, :], op0=ALU.add, op1=ALU.mult,
             )
             nc.vector.scalar_tensor_tensor(
                 out=cubes[:, 2, :], in0=xf, scalar=0.2, in1=x_sq[:, 1, :], op0=ALU.subtract, op1=ALU.mult,
             )
-            live[("cubes", q)] = cubes
+            live[("cubes", e)] = cubes
 
-        def vector_rest(q):
-            x_sq, dist, dist_sq, half_p, p_sq = live[("act", q)]
-            cubes = live[("cubes", q)]
-            if q == 0:
+        def vector_rest(e):
+            size = SIZES[e]
+            n = PASSES * size * PACK
+            x_sq, dist, dist_sq, half_p, p_sq = live[("act", e)]
+            cubes = live[("cubes", e)]
+            if e == 0:
                 regroup_g(0)
-            hump_raw = vpool.tile([P, 2, N], F32, name="hump_raw")
+            hump_raw = vone.tile([P, 2, n], F32, name="hump_raw")
             nc.vector.scalar_tensor_tensor(
                 out=hump_raw[:, 0, :], in0=half_p[:], scalar=1.0, in1=p_sq[:, 0, :],
                 op0=ALU.subtract, op1=ALU.mult,
@@ -132,14 +139,16 @@ def tile_kanlayer_kernel(tc, x, base_weight, spline_weight, grad_out, out):
                 out=hump_raw[:, 1, :], in0=half_p[:], scalar=0.5, in1=p_sq[:, 1, :],
                 op0=ALU.add, op1=ALU.mult,
             )
-            if q == 0:
+            if e == 0:
                 regroup_g(1)
+            if e + 2 in ON_VECTOR:
+                regroup(e + 2)
             nc.vector.scalar_tensor_tensor(
                 out=cubes[:, 0:4:3, :], in0=dist[:], scalar=2.0, in1=dist_sq[:],
                 op0=ALU.subtract, op1=ALU.mult,
             )
-            parts = vpool.tile([P, SPL, N], BF16, name="parts")
-            hump = vpool.tile([P, 2, N], BF16, name="hump")
+            parts = vone.tile([P, SPL, n], BF16, name="parts", tag="parts")
+            hump = vone.tile([P, 2, n], BF16, name="hump")
             nc.vector.tensor_scalar(
                 out=hump[:, 0, :], in0=hump_raw[:, 0, :], scalar1=TWO3, scalar2=None, op0=ALU.add,
             )
@@ -161,7 +170,7 @@ def tile_kanlayer_kernel(tc, x, base_weight, spline_weight, grad_out, out):
                 out=parts[:, 4, :], in0=cubes[:, 0, :], scalar1=-1.0, scalar2=0.0,
                 op0=ALU.mult, op1=ALU.max,
             )
-            basis = vpool.tile([P, PASSES, IC, SPL, PACK], BF16, name="basis", align_bytes=64)
+            basis = vtwo.tile([P, PASSES, size, SPL, PACK], BF16, name="basis", align_bytes=64)
             for h in (1, 3, 0, 2):
                 nc.vector.tensor_tensor(
                     out=basis[:, :, :, 2 * h : 2 * h + 2, :].rearrange("p c i l j -> p (c i) l j"),
@@ -169,13 +178,14 @@ def tile_kanlayer_kernel(tc, x, base_weight, spline_weight, grad_out, out):
                     in1=hump[:].rearrange("p r (n j) -> p n r j", j=PACK),
                     op=ALU.min,
                 )
-            live[("basis", q)] = basis
+            live[("basis", e)] = basis
 
-        def quantise(q):
-            basis = live[("basis", q)]
-            b_codes = cpool.tile([P, PASSES, W], U32, name="b_codes", align_bytes=64)
-            b_scales = cpool.tile([P, PASSES, W], U8, name="b_scales", align_bytes=64)
-            if q == NCH - 1:
+        def quantise(e):
+            size = SIZES[e]
+            basis = live[("basis", e)]
+            b_codes = cpool.tile([P, PASSES, size * SPL], U32, name="b_codes", align_bytes=64)
+            b_scales = cpool.tile([P, PASSES, size * SPL], U8, name="b_scales", align_bytes=64)
+            if size > GRP or e == nch - 1:
                 for c in range(PASSES):
                     nc.vector.quantize_mx(
                         out=b_codes[:, c, :].bitcast(E4),
@@ -188,28 +198,30 @@ def tile_kanlayer_kernel(tc, x, base_weight, spline_weight, grad_out, out):
                     scales=b_scales[:].rearrange("p c w -> p (c w)"),
                     in_=basis[:].rearrange("p c i l j -> p (c i l j)"),
                 )
-            live[("codes", q)] = (b_codes, b_scales)
+            live[("codes", e)] = (b_codes, b_scales)
 
-        def multiply(q):
-            b_codes, b_scales = live[("codes", q)]
-            banks = [psum.tile([P, W], F32, name="acc") for t in range(OT)]
-            for c in range(PASSES):
-                for t in range(OT):
-                    nc.tensor.matmul_mx(
-                        out=banks[t][:],
-                        lhsT=g_codes[:, c, t * P : (t + 1) * P].bitcast(E5),
-                        lhsT_scale=g_scales[:, c, t * P : (t + 1) * P],
-                        rhs=b_codes[:, c, :].bitcast(E4),
-                        rhs_scale=b_scales[:, c, :],
-                        start=(c == 0),
-                        stop=(c == PASSES - 1),
-                    )
-            live[("banks", q)] = banks
+        def multiply(e):
+            b_codes, b_scales = live[("codes", e)]
+            for k in range(SIZES[e] // GRP):
+                banks = [psum.tile([P, W], F32, name="acc") for t in range(OT)]
+                for c in range(PASSES):
+                    for t in range(OT):
+                        nc.tensor.matmul_mx(
+                            out=banks[t][:],
+                            lhsT=g_codes[:, c, t * P : (t + 1) * P].bitcast(E5),
+                            lhsT_scale=g_scales[:, c, t * P : (t + 1) * P],
+                            rhs=b_codes[:, c, k * W : (k + 1) * W].bitcast(E4),
+                            rhs_scale=b_scales[:, c, k * W : (k + 1) * W],
+                            start=(c == 0),
+                            stop=(c == PASSES - 1),
+                        )
+                live[("banks", e, k)] = banks
 
-        def empty(q, last):
-            banks = live[("banks", q)]
+        def empty(e, k, last):
+            banks = live[("banks", e, k)]
             res = stage.tile([P, OT, W], F32, name="res")
-            cols = slice(q * W, (q + 1) * W)
+            first_col = (starts[e] + k * GRP) * SPL
+            cols = slice(first_col, first_col + W)
             for t in range(OT):
                 if last and t % 2 == 1:
                     nc.vector.tensor_copy(out=res[:, t, :], in_=banks[t][:])
@@ -224,22 +236,22 @@ def tile_kanlayer_kernel(tc, x, base_weight, spline_weight, grad_out, out):
         scalar_part(0)
         regroup(1)
         scalar_part(1)
-        regroup(2)
         vector_first(0)
-        for q in range(NCH):
-            vector_rest(q)
-            if q + 1 < NCH:
-                vector_first(q + 1)
-            quantise(q)
-            if q == 0:
+        for e in range(nch):
+            vector_rest(e)
+            if e + 1 < nch:
+                vector_first(e + 1)
+            quantise(e)
+            if e == 0:
                 nc.vector.quantize_mx(
                     out=g_codes[:].rearrange("p c o -> p (c o)").bitcast(E5),
                     scales=g_scales[:].rearrange("p c o -> p (c o)"),
                     in_=g_grp[:].rearrange("p c o j -> p (c o j)"),
                 )
-            multiply(q)
-            if q + 2 < NCH:
-                scalar_part(q + 2)
-            if q + 3 < NCH:
-                regroup(q + 3)
-            empty(q, q == NCH - 1)
+            multiply(e)
+            if e + 2 < nch:
+                if e + 2 not in ON_VECTOR:
+                    regroup(e + 2)
+                scalar_part(e + 2)
+            for k in range(SIZES[e] // GRP):
+                empty(e, k, e == nch - 1)

@@ -23,6 +23,7 @@ OUTS = 512
 SPL = 8
 GRP = 64
 W = GRP * SPL
+M = GRP * PACK
 SIZES = (64, 128, 128, 128, 64)
 ON_VECTOR = (0, 1, 2)
 OT = OUTS // P
@@ -54,7 +55,7 @@ def tile_kanlayer_kernel(tc, x, base_weight, spline_weight, grad_out, out):
 
         x_head = keep.tile([P, PASSES, PACK, head], BF16)
         x_rest = keep.tile([P, PASSES, PACK, FEAT - head], BF16)
-        g_raw = vone.tile([P, PASSES, PACK, OUTS], BF16, tag="parts")
+        g_raw = vone.tile([P, PASSES, PACK, OUTS], BF16, name="g_raw")
         for c in range(PASSES):
             nc.sync.dma_start(out=x_head[:, c], in_=x_v[:, c, :, 0:head])
         for c in range(PASSES):
@@ -147,42 +148,42 @@ def tile_kanlayer_kernel(tc, x, base_weight, spline_weight, grad_out, out):
                 out=cubes[:, 0:4:3, :], in0=dist[:], scalar=2.0, in1=dist_sq[:],
                 op0=ALU.subtract, op1=ALU.mult,
             )
-            parts = vone.tile([P, SPL, n], BF16, name="parts", tag="parts")
             hump = vone.tile([P, 2, n], BF16, name="hump")
             nc.vector.tensor_scalar(
-                out=hump[:, 0, :], in0=hump_raw[:, 0, :], scalar1=TWO3, scalar2=None, op0=ALU.add,
+                out=hump[:, 1, :], in0=hump_raw[:, 0, :], scalar1=TWO3, scalar2=None, op0=ALU.add,
             )
             nc.vector.tensor_scalar(
-                out=hump[:, 1, :], in0=hump_raw[:, 1, :], scalar1=-1.0, scalar2=TWO3,
+                out=hump[:, 0, :], in0=hump_raw[:, 1, :], scalar1=-1.0, scalar2=TWO3,
                 op0=ALU.mult, op1=ALU.add,
             )
+            blocks = PASSES * size // GRP
+            basis = vtwo.tile([P, blocks, SPL, M], BF16, name="basis", align_bytes=64)
+            cubes_v = cubes[:].rearrange("p q (a m) -> p a q m", m=M)
             nc.vector.tensor_scalar(
-                out=parts[:, 1:4, :], in0=cubes[:, 1:4, :], scalar1=-1.0, scalar2=0.0,
+                out=basis[:, :, 4, :], in0=cubes_v[:, :, 0, :], scalar1=-1.0, scalar2=0.0,
                 op0=ALU.mult, op1=ALU.max,
             )
             nc.vector.tensor_scalar(
-                out=parts[:, 5:8, :], in0=cubes[:, 1:4, :], scalar1=0.0, scalar2=None, op0=ALU.max,
-            )
-            nc.vector.tensor_scalar(
-                out=parts[:, 0, :], in0=cubes[:, 0, :], scalar1=0.0, scalar2=None, op0=ALU.max,
-            )
-            nc.vector.tensor_scalar(
-                out=parts[:, 4, :], in0=cubes[:, 0, :], scalar1=-1.0, scalar2=0.0,
+                out=basis[:, :, 1:4, :], in0=cubes_v[:, :, 1:4, :], scalar1=-1.0, scalar2=0.0,
                 op0=ALU.mult, op1=ALU.max,
             )
-            basis = vtwo.tile([P, PASSES, size, SPL, PACK], BF16, name="basis", align_bytes=64)
-            for h in (1, 3, 0, 2):
+            nc.vector.tensor_scalar(
+                out=basis[:, :, 5:8, :], in0=cubes_v[:, :, 1:4, :], scalar1=0.0, scalar2=None, op0=ALU.max,
+            )
+            nc.vector.tensor_scalar(
+                out=basis[:, :, 0, :], in0=cubes_v[:, :, 0, :], scalar1=0.0, scalar2=None, op0=ALU.max,
+            )
+            hump_v = hump[:].rearrange("p r (a m) -> p a r m", m=M)
+            for l in (1, 3, 5):
                 nc.vector.tensor_tensor(
-                    out=basis[:, :, :, 2 * h : 2 * h + 2, :].rearrange("p c i l j -> p (c i) l j"),
-                    in0=parts[:, 2 * h : 2 * h + 2, :].rearrange("p l (n j) -> p n l j", j=PACK),
-                    in1=hump[:].rearrange("p r (n j) -> p n r j", j=PACK),
-                    op=ALU.min,
+                    out=basis[:, :, l : l + 2, :], in0=basis[:, :, l : l + 2, :], in1=hump_v, op=ALU.min,
                 )
             live[("basis", e)] = basis
 
         def quantise(e):
             size = SIZES[e]
             basis = live[("basis", e)]
+            per = size // GRP
             b_codes = cpool.tile([P, PASSES, size * SPL], U32, name="b_codes", align_bytes=64)
             b_scales = cpool.tile([P, PASSES, size * SPL], U8, name="b_scales", align_bytes=64)
             if size > GRP or e == nch - 1:
@@ -190,13 +191,13 @@ def tile_kanlayer_kernel(tc, x, base_weight, spline_weight, grad_out, out):
                     nc.vector.quantize_mx(
                         out=b_codes[:, c, :].bitcast(E4),
                         scales=b_scales[:, c, :],
-                        in_=basis[:, c].rearrange("p i l j -> p (i l j)"),
+                        in_=basis[:, c * per : (c + 1) * per].rearrange("p k l m -> p (k l m)"),
                     )
             else:
                 nc.vector.quantize_mx(
                     out=b_codes[:].rearrange("p c w -> p (c w)").bitcast(E4),
                     scales=b_scales[:].rearrange("p c w -> p (c w)"),
-                    in_=basis[:].rearrange("p c i l j -> p (c i l j)"),
+                    in_=basis[:].rearrange("p a l m -> p (a l m)"),
                 )
             live[("codes", e)] = (b_codes, b_scales)
 
@@ -224,9 +225,15 @@ def tile_kanlayer_kernel(tc, x, base_weight, spline_weight, grad_out, out):
             cols = slice(first_col, first_col + W)
             for t in range(OT):
                 if last and t % 2 == 1:
-                    nc.vector.tensor_copy(out=res[:, t, :], in_=banks[t][:])
+                    nc.vector.tensor_copy(
+                        out=res[:, t, :].rearrange("p (i l) -> p i l", l=SPL),
+                        in_=banks[t][:].rearrange("p (l i) -> p i l", l=SPL),
+                    )
                 else:
-                    nc.scalar.copy(out=res[:, t, :], in_=banks[t][:])
+                    nc.scalar.copy(
+                        out=res[:, t, :].rearrange("p (i l) -> p i l", l=SPL),
+                        in_=banks[t][:].rearrange("p (l i) -> p i l", l=SPL),
+                    )
                 if last and t % 2 == 1:
                     nc.sync.dma_start(out=out_v[:, t - 1 : t + 1, cols], in_=res[:, t - 1 : t + 1, :])
             if not last:

@@ -2,6 +2,7 @@ import math
 from contextlib import ExitStack
 
 import concourse.mybir as mybir
+from concourse.masks import make_identity
 
 FLOPS = 2 * 1024 * 512 * 4096
 BYTES = 2 * 1024 * 512 * 2 + 512 * 4096 * 4
@@ -25,8 +26,9 @@ GRP = 64
 W = GRP * SPL
 M = GRP * PACK
 SIZES = (64, 128, 128, 128, 64)
-ON_VECTOR = (0, 1, 2)
+BANK = 512
 OT = OUTS // P
+GH = 2
 
 K6 = 1.0 / math.sqrt(6.0)
 SX = math.sqrt(2.5 ** 3 / 6.0)
@@ -45,13 +47,16 @@ def tile_kanlayer_kernel(tc, x, base_weight, spline_weight, grad_out, out):
     with ExitStack() as ctx:
         ctx.enter_context(tc.manual_schedule())
         keep = ctx.enter_context(tc.tile_pool(name="keep", bufs=1))
-        xgp = ctx.enter_context(tc.tile_pool(name="xgp", bufs=3))
         apool = ctx.enter_context(tc.tile_pool(name="apool", bufs=2))
         vone = ctx.enter_context(tc.tile_pool(name="vone", bufs=1))
         vtwo = ctx.enter_context(tc.tile_pool(name="vtwo", bufs=2))
         cpool = ctx.enter_context(tc.tile_pool(name="cpool", bufs=2))
         stage = ctx.enter_context(tc.tile_pool(name="stage", bufs=3))
-        psum = ctx.enter_context(tc.psum_pool(name="psum", bufs=8))
+        psum = ctx.enter_context(tc.psum_pool(name="psum", bufs=4))
+        xpsum = ctx.enter_context(tc.psum_pool(name="xpsum", bufs=4))
+
+        ident = keep.tile([P, P], BF16)
+        make_identity(nc, ident[:])
 
         x_head = keep.tile([P, PASSES, PACK, head], BF16)
         x_rest = keep.tile([P, PASSES, PACK, FEAT - head], BF16)
@@ -59,9 +64,11 @@ def tile_kanlayer_kernel(tc, x, base_weight, spline_weight, grad_out, out):
         for c in range(PASSES):
             nc.sync.dma_start(out=x_head[:, c], in_=x_v[:, c, :, 0:head])
         for c in range(PASSES):
-            nc.sync.dma_start(out=x_rest[:, c], in_=x_v[:, c, :, head:FEAT])
+            for h in range(GH):
+                cols = slice(h * OUTS // GH, (h + 1) * OUTS // GH)
+                nc.sync.dma_start(out=g_raw[:, c, :, cols], in_=g_v[:, c, :, cols])
         for c in range(PASSES):
-            nc.sync.dma_start(out=g_raw[:, c], in_=g_v[:, c])
+            nc.sync.dma_start(out=x_rest[:, c], in_=x_v[:, c, :, head:FEAT])
 
         g_grp = keep.tile([P, PASSES, OUTS, PACK], BF16, align_bytes=64)
         g_codes = keep.tile([P, PASSES, OUTS], U32, align_bytes=64)
@@ -75,15 +82,17 @@ def tile_kanlayer_kernel(tc, x, base_weight, spline_weight, grad_out, out):
                 src = x_head[:]
             else:
                 src = x_rest[:, :, :, starts[e] - head : starts[e] - head + size]
-            xg = xgp.tile([P, PASSES, size, PACK], BF16, name="xg")
-            if e in ON_VECTOR:
-                nc.vector.tensor_copy(
-                    out=xg[:].rearrange("p c (a b) j -> p c a j b", b=4),
-                    in_=src.rearrange("p c j (a b) -> p c a j b", b=4),
-                )
-            else:
-                nc.scalar.copy(out=xg[:], in_=src.rearrange("p c j i -> p c i j"))
-            live[("xf", e)] = xg[:].rearrange("p c i j -> p (c i j)")
+            wide = size * PACK
+            banks = [xpsum.tile([P, BANK], F32, name="xp") for b in range(PASSES * wide // BANK)]
+            for c in range(PASSES):
+                first = c * wide
+                dst = banks[first // BANK][:, first % BANK : first % BANK + wide]
+                for j in range(PACK):
+                    nc.tensor.matmul(
+                        out=dst.rearrange("p (i j) -> p i j", j=PACK)[:, :, j],
+                        lhsT=ident[:], rhs=src[:, c, j, :], start=True, stop=True,
+                    )
+            live[("xf", e)] = banks
 
         def scalar_part(e):
             n = PASSES * SIZES[e] * PACK
@@ -94,34 +103,46 @@ def tile_kanlayer_kernel(tc, x, base_weight, spline_weight, grad_out, out):
             fold = apool.tile([P, n], F32, name="fold")
             half_p = apool.tile([P, n], F32, name="half_p")
             p_sq = apool.tile([P, 2, n], F32, name="p_sq")
-            nc.scalar.activation(out=dist[:, 0, :], in_=xf, func=ACT.Abs, bias=-0.5, scale=2.5)
-            nc.scalar.activation(out=x_sq[:, 0, :], in_=xf, func=ACT.Square, bias=0.2 * SX, scale=SX)
+
+            def of_x(plane, func, bias, scale):
+                for b, bank in enumerate(xf):
+                    nc.scalar.activation(
+                        out=plane[:, b * BANK : (b + 1) * BANK], in_=bank[:], func=func, bias=bias, scale=scale,
+                    )
+
+            of_x(x_sq[:, 0, :], ACT.Square, 0.2 * SX, SX)
+            of_x(x_sq[:, 1, :], ACT.Square, -0.2 * SX, SX)
+            of_x(dist[:, 0, :], ACT.Abs, -0.5, 2.5)
+            of_x(dist[:, 1, :], ACT.Abs, 0.5, 2.5)
             nc.scalar.activation(out=fold[:], in_=dist[:, 0, :], func=ACT.Abs, bias=-1.0, scale=1.0)
-            nc.scalar.activation(out=x_sq[:, 1, :], in_=xf, func=ACT.Square, bias=-0.2 * SX, scale=SX)
+            nc.scalar.activation(out=dist_sq[:], in_=dist[:], func=ACT.Square, bias=-2.0 * K6, scale=K6)
             nc.scalar.activation(out=half_p[:], in_=fold[:], func=ACT.Abs, bias=-0.5, scale=0.5)
-            nc.scalar.activation(out=dist[:, 1, :], in_=xf, func=ACT.Abs, bias=0.5, scale=2.5)
             nc.scalar.activation(out=p_sq[:, 0, :], in_=fold[:], func=ACT.Square, bias=-1.0, scale=1.0)
             nc.scalar.activation(out=p_sq[:, 1, :], in_=half_p[:], func=ACT.Square, bias=1.0, scale=-2.0)
-            nc.scalar.activation(out=dist_sq[:], in_=dist[:], func=ACT.Square, bias=-2.0 * K6, scale=K6)
             live[("act", e)] = (x_sq, dist, dist_sq, half_p, p_sq)
 
         def regroup_g(c):
-            nc.vector.tensor_copy(
-                out=g_grp[:, c].rearrange("p (a b) j -> p a j b", b=4),
-                in_=g_raw[:, c].rearrange("p j (a b) -> p a j b", b=4),
-            )
+            for h in range(GH):
+                cols = slice(h * OUTS // GH, (h + 1) * OUTS // GH)
+                nc.vector.tensor_copy(
+                    out=g_grp[:, c, cols, :].rearrange("p (a b) j -> p a j b", b=4),
+                    in_=g_raw[:, c, :, cols].rearrange("p j (a b) -> p a j b", b=4),
+                )
 
         def vector_first(e):
             n = PASSES * SIZES[e] * PACK
             xf = live[("xf", e)]
             x_sq = live[("act", e)][0]
             cubes = vtwo.tile([P, 4, n], BF16, name="cubes")
-            nc.vector.scalar_tensor_tensor(
-                out=cubes[:, 1, :], in0=xf, scalar=0.2, in1=x_sq[:, 0, :], op0=ALU.add, op1=ALU.mult,
-            )
-            nc.vector.scalar_tensor_tensor(
-                out=cubes[:, 2, :], in0=xf, scalar=0.2, in1=x_sq[:, 1, :], op0=ALU.subtract, op1=ALU.mult,
-            )
+            for b, bank in enumerate(xf):
+                cols = slice(b * BANK, (b + 1) * BANK)
+                nc.vector.scalar_tensor_tensor(
+                    out=cubes[:, 1, cols], in0=bank[:], scalar=0.2, in1=x_sq[:, 0, cols], op0=ALU.add, op1=ALU.mult,
+                )
+                nc.vector.scalar_tensor_tensor(
+                    out=cubes[:, 2, cols], in0=bank[:], scalar=0.2, in1=x_sq[:, 1, cols],
+                    op0=ALU.subtract, op1=ALU.mult,
+                )
             live[("cubes", e)] = cubes
 
         def vector_rest(e):
@@ -129,8 +150,10 @@ def tile_kanlayer_kernel(tc, x, base_weight, spline_weight, grad_out, out):
             n = PASSES * size * PACK
             x_sq, dist, dist_sq, half_p, p_sq = live[("act", e)]
             cubes = live[("cubes", e)]
-            if e == 0:
-                regroup_g(0)
+            nc.vector.scalar_tensor_tensor(
+                out=cubes[:, 0:4:3, :], in0=dist[:], scalar=2.0, in1=dist_sq[:],
+                op0=ALU.subtract, op1=ALU.mult,
+            )
             hump_raw = vone.tile([P, 2, n], F32, name="hump_raw")
             nc.vector.scalar_tensor_tensor(
                 out=hump_raw[:, 0, :], in0=half_p[:], scalar=1.0, in1=p_sq[:, 0, :],
@@ -139,14 +162,6 @@ def tile_kanlayer_kernel(tc, x, base_weight, spline_weight, grad_out, out):
             nc.vector.scalar_tensor_tensor(
                 out=hump_raw[:, 1, :], in0=half_p[:], scalar=0.5, in1=p_sq[:, 1, :],
                 op0=ALU.add, op1=ALU.mult,
-            )
-            if e == 0:
-                regroup_g(1)
-            if e + 2 in ON_VECTOR:
-                regroup(e + 2)
-            nc.vector.scalar_tensor_tensor(
-                out=cubes[:, 0:4:3, :], in0=dist[:], scalar=2.0, in1=dist_sq[:],
-                op0=ALU.subtract, op1=ALU.mult,
             )
             hump = vone.tile([P, 2, n], BF16, name="hump")
             nc.vector.tensor_scalar(
@@ -201,22 +216,24 @@ def tile_kanlayer_kernel(tc, x, base_weight, spline_weight, grad_out, out):
                 )
             live[("codes", e)] = (b_codes, b_scales)
 
-        def multiply(e):
+        def multiply(e, k):
             b_codes, b_scales = live[("codes", e)]
-            for k in range(SIZES[e] // GRP):
-                banks = [psum.tile([P, W], F32, name="acc") for t in range(OT)]
-                for c in range(PASSES):
-                    for t in range(OT):
-                        nc.tensor.matmul_mx(
-                            out=banks[t][:],
-                            lhsT=g_codes[:, c, t * P : (t + 1) * P].bitcast(E5),
-                            lhsT_scale=g_scales[:, c, t * P : (t + 1) * P],
-                            rhs=b_codes[:, c, k * W : (k + 1) * W].bitcast(E4),
-                            rhs_scale=b_scales[:, c, k * W : (k + 1) * W],
-                            start=(c == 0),
-                            stop=(c == PASSES - 1),
-                        )
-                live[("banks", e, k)] = banks
+            banks = [psum.tile([P, W], F32, name="acc") for t in range(OT)]
+            if e == nch - 1:
+                order = [(c, t) for c in range(PASSES) for t in range(OT)]
+            else:
+                order = [(c, t) for t in range(OT) for c in range(PASSES)]
+            for c, t in order:
+                nc.tensor.matmul_mx(
+                    out=banks[t][:],
+                    lhsT=g_codes[:, c, t * P : (t + 1) * P].bitcast(E5),
+                    lhsT_scale=g_scales[:, c, t * P : (t + 1) * P],
+                    rhs=b_codes[:, c, k * W : (k + 1) * W].bitcast(E4),
+                    rhs_scale=b_scales[:, c, k * W : (k + 1) * W],
+                    start=(c == 0),
+                    stop=(c == PASSES - 1),
+                )
+            live[("banks", e, k)] = banks
 
         def empty(e, k, last):
             banks = live[("banks", e, k)]
@@ -240,25 +257,26 @@ def tile_kanlayer_kernel(tc, x, base_weight, spline_weight, grad_out, out):
                 nc.sync.dma_start(out=out_v[:, :, cols], in_=res[:])
 
         regroup(0)
-        scalar_part(0)
         regroup(1)
+        scalar_part(0)
         scalar_part(1)
+        regroup_g(0)
+        regroup_g(1)
         vector_first(0)
+        nc.vector.quantize_mx(
+            out=g_codes[:].rearrange("p c o -> p (c o)").bitcast(E5),
+            scales=g_scales[:].rearrange("p c o -> p (c o)"),
+            in_=g_grp[:].rearrange("p c o j -> p (c o j)"),
+        )
         for e in range(nch):
             vector_rest(e)
             if e + 1 < nch:
                 vector_first(e + 1)
-            quantise(e)
-            if e == 0:
-                nc.vector.quantize_mx(
-                    out=g_codes[:].rearrange("p c o -> p (c o)").bitcast(E5),
-                    scales=g_scales[:].rearrange("p c o -> p (c o)"),
-                    in_=g_grp[:].rearrange("p c o j -> p (c o j)"),
-                )
-            multiply(e)
             if e + 2 < nch:
-                if e + 2 not in ON_VECTOR:
-                    regroup(e + 2)
+                regroup(e + 2)
+            quantise(e)
+            if e + 2 < nch:
                 scalar_part(e + 2)
             for k in range(SIZES[e] // GRP):
+                multiply(e, k)
                 empty(e, k, e == nch - 1)

@@ -29,6 +29,7 @@ SIZES = (64, 128, 128, 128, 64)
 BANK = 512
 OT = OUTS // P
 GH = 2
+G0 = 2
 
 K6 = 1.0 / math.sqrt(6.0)
 SX = math.sqrt(2.5 ** 3 / 6.0)
@@ -94,7 +95,7 @@ def tile_kanlayer_kernel(tc, x, base_weight, spline_weight, grad_out, out):
                     )
             live[("xf", e)] = banks
 
-        def scalar_part(e):
+        def scalar_reads(e):
             n = PASSES * SIZES[e] * PACK
             xf = live[("xf", e)]
             x_sq = apool.tile([P, 2, n], F32, name="x_sq")
@@ -114,12 +115,17 @@ def tile_kanlayer_kernel(tc, x, base_weight, spline_weight, grad_out, out):
             of_x(x_sq[:, 1, :], ACT.Square, -0.2 * SX, SX)
             of_x(dist[:, 0, :], ACT.Abs, -0.5, 2.5)
             of_x(dist[:, 1, :], ACT.Abs, 0.5, 2.5)
+            live[("act", e)] = (x_sq, dist, dist_sq, half_p, p_sq)
+            live[("fold", e)] = fold
+
+        def scalar_rest(e):
+            x_sq, dist, dist_sq, half_p, p_sq = live[("act", e)]
+            fold = live[("fold", e)]
             nc.scalar.activation(out=fold[:], in_=dist[:, 0, :], func=ACT.Abs, bias=-1.0, scale=1.0)
             nc.scalar.activation(out=dist_sq[:], in_=dist[:], func=ACT.Square, bias=-2.0 * K6, scale=K6)
             nc.scalar.activation(out=half_p[:], in_=fold[:], func=ACT.Abs, bias=-0.5, scale=0.5)
             nc.scalar.activation(out=p_sq[:, 0, :], in_=fold[:], func=ACT.Square, bias=-1.0, scale=1.0)
             nc.scalar.activation(out=p_sq[:, 1, :], in_=half_p[:], func=ACT.Square, bias=1.0, scale=-2.0)
-            live[("act", e)] = (x_sq, dist, dist_sq, half_p, p_sq)
 
         def regroup_g(c):
             for h in range(GH):
@@ -129,11 +135,17 @@ def tile_kanlayer_kernel(tc, x, base_weight, spline_weight, grad_out, out):
                     in_=g_raw[:, c, :, cols].rearrange("p j (a b) -> p a j b", b=4),
                 )
 
+        def cubes_of(e):
+            if ("cubes", e) not in live:
+                cubes = vtwo.tile([P, 4, PASSES * SIZES[e] * PACK], BF16, name="cubes")
+                live[("cubes", e)] = cubes
+            return live[("cubes", e)]
+
         def vector_first(e):
             n = PASSES * SIZES[e] * PACK
             xf = live[("xf", e)]
             x_sq = live[("act", e)][0]
-            cubes = vtwo.tile([P, 4, n], BF16, name="cubes")
+            cubes = cubes_of(e)
             for b, bank in enumerate(xf):
                 cols = slice(b * BANK, (b + 1) * BANK)
                 nc.vector.scalar_tensor_tensor(
@@ -143,17 +155,18 @@ def tile_kanlayer_kernel(tc, x, base_weight, spline_weight, grad_out, out):
                     out=cubes[:, 2, cols], in0=bank[:], scalar=0.2, in1=x_sq[:, 1, cols],
                     op0=ALU.subtract, op1=ALU.mult,
                 )
-            live[("cubes", e)] = cubes
 
-        def vector_rest(e):
-            size = SIZES[e]
-            n = PASSES * size * PACK
+        def far_cubes(e):
             x_sq, dist, dist_sq, half_p, p_sq = live[("act", e)]
-            cubes = live[("cubes", e)]
+            cubes = cubes_of(e)
             nc.vector.scalar_tensor_tensor(
                 out=cubes[:, 0:4:3, :], in0=dist[:], scalar=2.0, in1=dist_sq[:],
                 op0=ALU.subtract, op1=ALU.mult,
             )
+
+        def hump_products(e):
+            n = PASSES * SIZES[e] * PACK
+            x_sq, dist, dist_sq, half_p, p_sq = live[("act", e)]
             hump_raw = vone.tile([P, 2, n], F32, name="hump_raw")
             nc.vector.scalar_tensor_tensor(
                 out=hump_raw[:, 0, :], in0=half_p[:], scalar=1.0, in1=p_sq[:, 0, :],
@@ -163,14 +176,35 @@ def tile_kanlayer_kernel(tc, x, base_weight, spline_weight, grad_out, out):
                 out=hump_raw[:, 1, :], in0=half_p[:], scalar=0.5, in1=p_sq[:, 1, :],
                 op0=ALU.add, op1=ALU.mult,
             )
+            live[("hump_raw", e)] = hump_raw
+
+        def round_humps(e):
+            n = PASSES * SIZES[e] * PACK
+            hump_raw = live[("hump_raw", e)]
             hump = vone.tile([P, 2, n], BF16, name="hump")
-            nc.vector.tensor_scalar(
-                out=hump[:, 1, :], in0=hump_raw[:, 0, :], scalar1=TWO3, scalar2=None, op0=ALU.add,
-            )
-            nc.vector.tensor_scalar(
-                out=hump[:, 0, :], in0=hump_raw[:, 1, :], scalar1=-1.0, scalar2=TWO3,
-                op0=ALU.mult, op1=ALU.add,
-            )
+            if e >= G0:
+                nc.gpsimd.tensor_scalar(
+                    out=hump[:, 0, :], in0=hump_raw[:, 1, :], scalar1=-1.0, scalar2=TWO3,
+                    op0=ALU.mult, op1=ALU.add,
+                )
+                nc.gpsimd.tensor_scalar(
+                    out=hump[:, 1, :], in0=hump_raw[:, 0, :], scalar1=1.0, scalar2=TWO3,
+                    op0=ALU.mult, op1=ALU.add,
+                )
+            else:
+                nc.vector.tensor_scalar(
+                    out=hump[:, 1, :], in0=hump_raw[:, 0, :], scalar1=TWO3, scalar2=None, op0=ALU.add,
+                )
+                nc.vector.tensor_scalar(
+                    out=hump[:, 0, :], in0=hump_raw[:, 1, :], scalar1=-1.0, scalar2=TWO3,
+                    op0=ALU.mult, op1=ALU.add,
+                )
+            live[("hump", e)] = hump
+
+        def select(e):
+            size = SIZES[e]
+            cubes = live[("cubes", e)]
+            hump = live[("hump", e)]
             blocks = PASSES * size // GRP
             basis = vtwo.tile([P, blocks, SPL, M], BF16, name="basis", align_bytes=64)
             cubes_v = cubes[:].rearrange("p q (a m) -> p a q m", m=M)
@@ -258,8 +292,10 @@ def tile_kanlayer_kernel(tc, x, base_weight, spline_weight, grad_out, out):
 
         regroup(0)
         regroup(1)
-        scalar_part(0)
-        scalar_part(1)
+        scalar_reads(0)
+        scalar_rest(0)
+        scalar_reads(1)
+        scalar_rest(1)
         regroup_g(0)
         regroup_g(1)
         vector_first(0)
@@ -268,15 +304,25 @@ def tile_kanlayer_kernel(tc, x, base_weight, spline_weight, grad_out, out):
             scales=g_scales[:].rearrange("p c o -> p (c o)"),
             in_=g_grp[:].rearrange("p c o j -> p (c o j)"),
         )
+        far_cubes(0)
         for e in range(nch):
-            vector_rest(e)
-            if e + 1 < nch:
+            hump_products(e)
+            round_humps(e)
+            if e >= G0:
+                vector_first(e)
+            select(e)
+            if e + 1 < G0:
                 vector_first(e + 1)
             if e + 2 < nch:
                 regroup(e + 2)
+            if e + 1 >= G0 and e + 1 < nch:
+                far_cubes(e + 1)
             quantise(e)
+            if e + 1 < G0:
+                far_cubes(e + 1)
             if e + 2 < nch:
-                scalar_part(e + 2)
+                scalar_reads(e + 2)
+                scalar_rest(e + 2)
             for k in range(SIZES[e] // GRP):
                 multiply(e, k)
                 empty(e, k, e == nch - 1)

@@ -223,11 +223,39 @@ def tile_kanlayer_kernel(tc, x, base_weight, spline_weight, grad_out, out):
                 out=basis[:, :, 0, :], in0=cubes_v[:, :, 0, :], scalar1=0.0, scalar2=None, op0=ALU.max,
             )
             hump_v = hump[:].rearrange("p r (a m) -> p a r m", m=M)
-            for l in (1, 3, 5):
-                nc.vector.tensor_tensor(
-                    out=basis[:, :, l : l + 2, :], in0=basis[:, :, l : l + 2, :], in1=hump_v, op=ALU.min,
-                )
             live[("basis", e)] = basis
+            if e < nch - 1:
+                for l in (1, 3, 5):
+                    nc.vector.tensor_tensor(
+                        out=basis[:, :, l : l + 2, :], in0=basis[:, :, l : l + 2, :], in1=hump_v, op=ALU.min,
+                    )
+                return
+
+            def clamp(c, l):
+                nc.vector.tensor_tensor(
+                    out=basis[:, c, l : l + 2, :], in0=basis[:, c, l : l + 2, :], in1=hump_v[:, c], op=ALU.min,
+                )
+
+            b_codes = cpool.tile([P, PASSES, W], U32, name="b_codes", align_bytes=64)
+            b_scales = cpool.tile([P, PASSES, W], U8, name="b_scales", align_bytes=64)
+            live[("codes", e)] = (b_codes, b_scales)
+
+            def pack(c, l0, l1):
+                nc.vector.quantize_mx(
+                    out=b_codes[:, c, l0 * GRP : l1 * GRP].bitcast(E4),
+                    scales=b_scales[:, c, l0 * GRP : l1 * GRP],
+                    in_=basis[:, c, l0:l1, :].rearrange("p l m -> p (l m)"),
+                )
+
+            clamp(0, 1)
+            clamp(0, 3)
+            clamp(0, 5)
+            clamp(1, 1)
+            clamp(1, 3)
+            pack(0, 0, SPL)
+            clamp(1, 5)
+            pack(1, 0, SPL // 2)
+            pack(1, SPL // 2, SPL)
 
         def quantise(e):
             size = SIZES[e]
@@ -235,7 +263,7 @@ def tile_kanlayer_kernel(tc, x, base_weight, spline_weight, grad_out, out):
             per = size // GRP
             b_codes = cpool.tile([P, PASSES, size * SPL], U32, name="b_codes", align_bytes=64)
             b_scales = cpool.tile([P, PASSES, size * SPL], U8, name="b_scales", align_bytes=64)
-            if size > GRP or e == nch - 1:
+            if size > GRP:
                 for c in range(PASSES):
                     nc.vector.quantize_mx(
                         out=b_codes[:, c, :].bitcast(E4),
@@ -317,7 +345,8 @@ def tile_kanlayer_kernel(tc, x, base_weight, spline_weight, grad_out, out):
                 regroup(e + 2)
             if e + 1 >= G0 and e + 1 < nch:
                 far_cubes(e + 1)
-            quantise(e)
+            if e < nch - 1:
+                quantise(e)
             if e + 1 < G0:
                 far_cubes(e + 1)
             if e + 2 < nch:

@@ -26,7 +26,6 @@ GRP = 64
 W = GRP * SPL
 M = GRP * PACK
 SIZES = (64, 128, 128, 128, 64)
-BANK = 512
 OT = OUTS // P
 GH = 2
 G0 = 2
@@ -54,7 +53,7 @@ def tile_kanlayer_kernel(tc, x, base_weight, spline_weight, grad_out, out):
         cpool = ctx.enter_context(tc.tile_pool(name="cpool", bufs=2))
         stage = ctx.enter_context(tc.tile_pool(name="stage", bufs=3))
         psum = ctx.enter_context(tc.psum_pool(name="psum", bufs=4))
-        xpsum = ctx.enter_context(tc.psum_pool(name="xpsum", bufs=4))
+        xpsum = ctx.enter_context(tc.psum_pool(name="xpsum", bufs=2))
 
         ident = keep.tile([P, P], BF16)
         make_identity(nc, ident[:])
@@ -84,16 +83,13 @@ def tile_kanlayer_kernel(tc, x, base_weight, spline_weight, grad_out, out):
             else:
                 src = x_rest[:, :, :, starts[e] - head : starts[e] - head + size]
             wide = size * PACK
-            banks = [xpsum.tile([P, BANK], F32, name="xp") for b in range(PASSES * wide // BANK)]
+            xp = xpsum.tile([P, PASSES * wide], BF16, name="xp")
             for c in range(PASSES):
-                first = c * wide
-                dst = banks[first // BANK][:, first % BANK : first % BANK + wide]
-                for j in range(PACK):
-                    nc.tensor.matmul(
-                        out=dst.rearrange("p (i j) -> p i j", j=PACK)[:, :, j],
-                        lhsT=ident[:], rhs=src[:, c, j, :], start=True, stop=True,
-                    )
-            live[("xf", e)] = banks
+                nc.tensor.matmul(
+                    out=xp[:, c * wide : (c + 1) * wide].rearrange("p (i j) -> p i j", j=PACK),
+                    lhsT=ident[:], rhs=src[:, c].rearrange("p j i -> p i j"), start=True, stop=True,
+                )
+            live[("xf", e)] = xp[:]
 
         def scalar_reads(e):
             n = PASSES * SIZES[e] * PACK
@@ -104,17 +100,10 @@ def tile_kanlayer_kernel(tc, x, base_weight, spline_weight, grad_out, out):
             fold = apool.tile([P, n], F32, name="fold")
             half_p = apool.tile([P, n], F32, name="half_p")
             p_sq = apool.tile([P, 2, n], F32, name="p_sq")
-
-            def of_x(plane, func, bias, scale):
-                for b, bank in enumerate(xf):
-                    nc.scalar.activation(
-                        out=plane[:, b * BANK : (b + 1) * BANK], in_=bank[:], func=func, bias=bias, scale=scale,
-                    )
-
-            of_x(x_sq[:, 0, :], ACT.Square, 0.2 * SX, SX)
-            of_x(x_sq[:, 1, :], ACT.Square, -0.2 * SX, SX)
-            of_x(dist[:, 0, :], ACT.Abs, -0.5, 2.5)
-            of_x(dist[:, 1, :], ACT.Abs, 0.5, 2.5)
+            nc.scalar.activation(out=x_sq[:, 0, :], in_=xf, func=ACT.Square, bias=0.2 * SX, scale=SX)
+            nc.scalar.activation(out=x_sq[:, 1, :], in_=xf, func=ACT.Square, bias=-0.2 * SX, scale=SX)
+            nc.scalar.activation(out=dist[:, 0, :], in_=xf, func=ACT.Abs, bias=-0.5, scale=2.5)
+            nc.scalar.activation(out=dist[:, 1, :], in_=xf, func=ACT.Abs, bias=0.5, scale=2.5)
             live[("act", e)] = (x_sq, dist, dist_sq, half_p, p_sq)
             live[("fold", e)] = fold
 
@@ -146,15 +135,12 @@ def tile_kanlayer_kernel(tc, x, base_weight, spline_weight, grad_out, out):
             xf = live[("xf", e)]
             x_sq = live[("act", e)][0]
             cubes = cubes_of(e)
-            for b, bank in enumerate(xf):
-                cols = slice(b * BANK, (b + 1) * BANK)
-                nc.vector.scalar_tensor_tensor(
-                    out=cubes[:, 1, cols], in0=bank[:], scalar=0.2, in1=x_sq[:, 0, cols], op0=ALU.add, op1=ALU.mult,
-                )
-                nc.vector.scalar_tensor_tensor(
-                    out=cubes[:, 2, cols], in0=bank[:], scalar=0.2, in1=x_sq[:, 1, cols],
-                    op0=ALU.subtract, op1=ALU.mult,
-                )
+            nc.vector.scalar_tensor_tensor(
+                out=cubes[:, 1, :], in0=xf, scalar=0.2, in1=x_sq[:, 0, :], op0=ALU.add, op1=ALU.mult,
+            )
+            nc.vector.scalar_tensor_tensor(
+                out=cubes[:, 2, :], in0=xf, scalar=0.2, in1=x_sq[:, 1, :], op0=ALU.subtract, op1=ALU.mult,
+            )
 
         def far_cubes(e):
             x_sq, dist, dist_sq, half_p, p_sq = live[("act", e)]

@@ -25,6 +25,7 @@ SPL = 8
 GRP = 64
 W = GRP * SPL
 M = GRP * PACK
+BANK = 512
 SIZES = (64, 128, 128, 128, 64)
 OT = OUTS // P
 GH = 2
@@ -54,9 +55,12 @@ def tile_kanlayer_kernel(tc, x, base_weight, spline_weight, grad_out, out):
         stage = ctx.enter_context(tc.tile_pool(name="stage", bufs=3))
         psum = ctx.enter_context(tc.psum_pool(name="psum", bufs=4))
         xpsum = ctx.enter_context(tc.psum_pool(name="xpsum", bufs=2))
+        dpsum = ctx.enter_context(tc.psum_pool(name="dpsum", bufs=2))
 
         ident = keep.tile([P, P], BF16)
         make_identity(nc, ident[:])
+        ident32 = keep.tile([P, P], F32)
+        make_identity(nc, ident32[:])
 
         x_head = keep.tile([P, PASSES, PACK, head], BF16)
         x_rest = keep.tile([P, PASSES, PACK, FEAT - head], BF16)
@@ -145,10 +149,38 @@ def tile_kanlayer_kernel(tc, x, base_weight, spline_weight, grad_out, out):
         def far_cubes(e):
             x_sq, dist, dist_sq, half_p, p_sq = live[("act", e)]
             cubes = cubes_of(e)
-            nc.vector.scalar_tensor_tensor(
-                out=cubes[:, 0:4:3, :], in0=dist[:], scalar=2.0, in1=dist_sq[:],
-                op0=ALU.subtract, op1=ALU.mult,
-            )
+            if e >= G0:
+                nc.vector.scalar_tensor_tensor(
+                    out=cubes[:, 0, :], in0=dist[:, 0, :], scalar=2.0, in1=dist_sq[:, 0, :],
+                    op0=ALU.subtract, op1=ALU.mult,
+                )
+            else:
+                nc.vector.scalar_tensor_tensor(
+                    out=cubes[:, 0:4:3, :], in0=dist[:], scalar=2.0, in1=dist_sq[:],
+                    op0=ALU.subtract, op1=ALU.mult,
+                )
+
+        def lift_distance(e):
+            n = PASSES * SIZES[e] * PACK
+            dist = live[("act", e)][1]
+            banks = []
+            for b in range(n // BANK):
+                dp = dpsum.tile([P, BANK], F32, name="dp")
+                nc.tensor.matmul(
+                    out=dp[:], lhsT=ident32[:], rhs=dist[:, 1, b * BANK : (b + 1) * BANK], start=True, stop=True,
+                )
+                banks.append(dp)
+            live[("dp", e)] = banks
+
+        def far_cube_from_psum(e):
+            dist_sq = live[("act", e)][2]
+            cubes = cubes_of(e)
+            for b, dp in enumerate(live[("dp", e)]):
+                cols = slice(b * BANK, (b + 1) * BANK)
+                nc.vector.scalar_tensor_tensor(
+                    out=cubes[:, 3, cols], in0=dp[:], scalar=2.0, in1=dist_sq[:, 1, cols],
+                    op0=ALU.subtract, op1=ALU.mult,
+                )
 
         def hump_products(e):
             n = PASSES * SIZES[e] * PACK
@@ -324,11 +356,14 @@ def tile_kanlayer_kernel(tc, x, base_weight, spline_weight, grad_out, out):
             round_humps(e)
             if e >= G0:
                 vector_first(e)
+                far_cube_from_psum(e)
+            if e + 2 < nch:
+                regroup(e + 2)
+            if e + 1 >= G0 and e + 1 < nch:
+                lift_distance(e + 1)
             select(e)
             if e + 1 < G0:
                 vector_first(e + 1)
-            if e + 2 < nch:
-                regroup(e + 2)
             if e + 1 >= G0 and e + 1 < nch:
                 far_cubes(e + 1)
             if e < nch - 1:

@@ -231,14 +231,14 @@ def tile_kanlayer_kernel(tc, x, base_weight, spline_weight, grad_out, out):
                 op0=ALU.mult, op1=ALU.max,
             )
             nc.vector.tensor_scalar(
+                out=basis[:, :, 0, :], in0=cubes_v[:, :, 0, :], scalar1=0.0, scalar2=None, op0=ALU.max,
+            )
+            nc.vector.tensor_scalar(
                 out=basis[:, :, 1:4, :], in0=cubes_v[:, :, 1:4, :], scalar1=-1.0, scalar2=0.0,
                 op0=ALU.mult, op1=ALU.max,
             )
             nc.vector.tensor_scalar(
                 out=basis[:, :, 5:8, :], in0=cubes_v[:, :, 1:4, :], scalar1=0.0, scalar2=None, op0=ALU.max,
-            )
-            nc.vector.tensor_scalar(
-                out=basis[:, :, 0, :], in0=cubes_v[:, :, 0, :], scalar1=0.0, scalar2=None, op0=ALU.max,
             )
             hump_v = hump[:].rearrange("p r (a m) -> p a r m", m=M)
             live[("basis", e)] = basis

@@ -205,10 +205,15 @@ def tile_kanlayer_kernel(tc, x, base_weight, spline_weight, grad_out, out):
                     out=hump[:, 0, :], in0=hump_raw[:, 1, :], scalar1=-1.0, scalar2=TWO3,
                     op0=ALU.mult, op1=ALU.add,
                 )
-                nc.gpsimd.tensor_scalar(
-                    out=hump[:, 1, :], in0=hump_raw[:, 0, :], scalar1=1.0, scalar2=TWO3,
-                    op0=ALU.mult, op1=ALU.add,
-                )
+                if e == nch - 1:
+                    nc.scalar.activation(
+                        out=hump[:, 1, :], in_=hump_raw[:, 0, :], func=ACT.Identity, bias=TWO3, scale=1.0,
+                    )
+                else:
+                    nc.gpsimd.tensor_scalar(
+                        out=hump[:, 1, :], in0=hump_raw[:, 0, :], scalar1=1.0, scalar2=TWO3,
+                        op0=ALU.mult, op1=ALU.add,
+                    )
             else:
                 nc.vector.tensor_scalar(
                     out=hump[:, 1, :], in0=hump_raw[:, 0, :], scalar1=TWO3, scalar2=None, op0=ALU.add,
@@ -219,20 +224,30 @@ def tile_kanlayer_kernel(tc, x, base_weight, spline_weight, grad_out, out):
                 )
             live[("hump", e)] = hump
 
+        def relu_far_on_scalar(e):
+            basis = vtwo.tile([P, PASSES * SIZES[e] // GRP, SPL, M], BF16, name="basis", align_bytes=64)
+            live[("basis", e)] = basis
+            cubes_v = live[("cubes", e)][:].rearrange("p q (a m) -> p a q m", m=M)
+            nc.scalar.activation(out=basis[:, :, 4, :], in_=cubes_v[:, :, 0, :], func=ACT.Relu, bias=0.0, scale=-1.0)
+            nc.scalar.activation(out=basis[:, :, 0, :], in_=cubes_v[:, :, 0, :], func=ACT.Relu, bias=0.0, scale=1.0)
+
         def select(e):
             size = SIZES[e]
             cubes = live[("cubes", e)]
             hump = live[("hump", e)]
             blocks = PASSES * size // GRP
-            basis = vtwo.tile([P, blocks, SPL, M], BF16, name="basis", align_bytes=64)
             cubes_v = cubes[:].rearrange("p q (a m) -> p a q m", m=M)
-            nc.vector.tensor_scalar(
-                out=basis[:, :, 4, :], in0=cubes_v[:, :, 0, :], scalar1=-1.0, scalar2=0.0,
-                op0=ALU.mult, op1=ALU.max,
-            )
-            nc.vector.tensor_scalar(
-                out=basis[:, :, 0, :], in0=cubes_v[:, :, 0, :], scalar1=0.0, scalar2=None, op0=ALU.max,
-            )
+            if e == nch - 1:
+                basis = live[("basis", e)]
+            else:
+                basis = vtwo.tile([P, blocks, SPL, M], BF16, name="basis", align_bytes=64)
+                nc.vector.tensor_scalar(
+                    out=basis[:, :, 4, :], in0=cubes_v[:, :, 0, :], scalar1=-1.0, scalar2=0.0,
+                    op0=ALU.mult, op1=ALU.max,
+                )
+                nc.vector.tensor_scalar(
+                    out=basis[:, :, 0, :], in0=cubes_v[:, :, 0, :], scalar1=0.0, scalar2=None, op0=ALU.max,
+                )
             nc.vector.tensor_scalar(
                 out=basis[:, :, 1:4, :], in0=cubes_v[:, :, 1:4, :], scalar1=-1.0, scalar2=0.0,
                 op0=ALU.mult, op1=ALU.max,
@@ -351,9 +366,9 @@ def tile_kanlayer_kernel(tc, x, base_weight, spline_weight, grad_out, out):
             in_=g_grp[:].rearrange("p c o j -> p (c o j)"),
         )
         far_cubes(0)
+        hump_products(0)
+        round_humps(0)
         for e in range(nch):
-            hump_products(e)
-            round_humps(e)
             if e >= G0:
                 vector_first(e)
                 far_cube_from_psum(e)
@@ -366,10 +381,15 @@ def tile_kanlayer_kernel(tc, x, base_weight, spline_weight, grad_out, out):
                 vector_first(e + 1)
             if e + 1 >= G0 and e + 1 < nch:
                 far_cubes(e + 1)
+            if e + 1 == nch - 1:
+                relu_far_on_scalar(e + 1)
             if e < nch - 1:
                 quantise(e)
             if e + 1 < G0:
                 far_cubes(e + 1)
+            if e + 1 < nch:
+                hump_products(e + 1)
+                round_humps(e + 1)
             if e + 2 < nch:
                 scalar_reads(e + 2)
                 scalar_rest(e + 2)

@@ -346,8 +346,8 @@ def tile_kanlayer_kernel(tc, x, base_weight, spline_weight, grad_out, out):
                         out=res[:, t, :].rearrange("p (i l) -> p i l", l=SPL),
                         in_=banks[t][:].rearrange("p (l i) -> p i l", l=SPL),
                     )
-                if last and t % 2 == 1:
-                    nc.sync.dma_start(out=out_v[:, t - 1 : t + 1, cols], in_=res[:, t - 1 : t + 1, :])
+                if last:
+                    nc.sync.dma_start(out=out_v[:, t, cols], in_=res[:, t, :])
             if not last:
                 nc.sync.dma_start(out=out_v[:, :, cols], in_=res[:])
 

import math
from contextlib import ExitStack

import concourse.mybir as mybir
from concourse.masks import make_identity

FLOPS = 2 * 1024 * 512 * 4096
BYTES = 2 * 1024 * 512 * 2 + 512 * 4096 * 4

BF16 = mybir.dt.bfloat16
F32 = mybir.dt.float32
U32 = mybir.dt.uint32
U8 = mybir.dt.uint8
E4 = mybir.dt.float8_e4m3fn_x4
E5 = mybir.dt.float8_e5m2_x4
ACT = mybir.ActivationFunctionType
ALU = mybir.AluOpType

P = 128
PASSES = 2
PACK = 4
FEAT = 512
OUTS = 512
SPL = 8
GRP = 64
W = GRP * SPL
M = GRP * PACK
BANK = 512
SIZES = (64, 128, 128, 128, 64)
OT = OUTS // P
GH = 2
G0 = 2

K6 = 1.0 / math.sqrt(6.0)
SX = math.sqrt(2.5 ** 3 / 6.0)
TWO3 = 2.0 / 3.0


def tile_kanlayer_kernel(tc, x, base_weight, spline_weight, grad_out, out):
    nc = tc.nc
    x_v = x.rearrange("(c p j) i -> p c j i", c=PASSES, p=P, j=PACK)
    g_v = grad_out.rearrange("(c p j) o -> p c j o", c=PASSES, p=P, j=PACK)
    out_v = out.rearrange("(t p) i l -> p t (i l)", p=P)
    nch = len(SIZES)
    starts = [sum(SIZES[:e]) for e in range(nch)]
    head = SIZES[0]

    with ExitStack() as ctx:
        ctx.enter_context(tc.manual_schedule())
        keep = ctx.enter_context(tc.tile_pool(name="keep", bufs=1))
        apool = ctx.enter_context(tc.tile_pool(name="apool", bufs=2))
        vone = ctx.enter_context(tc.tile_pool(name="vone", bufs=1))
        vtwo = ctx.enter_context(tc.tile_pool(name="vtwo", bufs=2))
        cpool = ctx.enter_context(tc.tile_pool(name="cpool", bufs=2))
        stage = ctx.enter_context(tc.tile_pool(name="stage", bufs=3))
        psum = ctx.enter_context(tc.psum_pool(name="psum", bufs=4))
        xpsum = ctx.enter_context(tc.psum_pool(name="xpsum", bufs=2))
        dpsum = ctx.enter_context(tc.psum_pool(name="dpsum", bufs=2))

        ident = keep.tile([P, P], BF16)
        make_identity(nc, ident[:])
        ident32 = keep.tile([P, P], F32)
        make_identity(nc, ident32[:])

        x_head = keep.tile([P, PASSES, PACK, head], BF16)
        x_rest = keep.tile([P, PASSES, PACK, FEAT - head], BF16)
        g_raw = vone.tile([P, PASSES, PACK, OUTS], BF16, name="g_raw")
        for c in range(PASSES):
            nc.sync.dma_start(out=x_head[:, c], in_=x_v[:, c, :, 0:head])
        for c in range(PASSES):
            for h in range(GH):
                cols = slice(h * OUTS // GH, (h + 1) * OUTS // GH)
                nc.sync.dma_start(out=g_raw[:, c, :, cols], in_=g_v[:, c, :, cols])
        for c in range(PASSES):
            nc.sync.dma_start(out=x_rest[:, c], in_=x_v[:, c, :, head:FEAT])

        g_grp = keep.tile([P, PASSES, OUTS, PACK], BF16, align_bytes=64)
        g_codes = keep.tile([P, PASSES, OUTS], U32, align_bytes=64)
        g_scales = keep.tile([P, PASSES, OUTS], U8, align_bytes=64)

        live = {}

        def regroup(e):
            size = SIZES[e]
            if e == 0:
                src = x_head[:]
            else:
                src = x_rest[:, :, :, starts[e] - head : starts[e] - head + size]
            wide = size * PACK
            xp = xpsum.tile([P, PASSES * wide], BF16, name="xp")
            for c in range(PASSES):
                nc.tensor.matmul(
                    out=xp[:, c * wide : (c + 1) * wide].rearrange("p (i j) -> p i j", j=PACK),
                    lhsT=ident[:], rhs=src[:, c].rearrange("p j i -> p i j"), start=True, stop=True,
                )
            live[("xf", e)] = xp[:]

        def scalar_reads(e):
            n = PASSES * SIZES[e] * PACK
            xf = live[("xf", e)]
            x_sq = apool.tile([P, 2, n], F32, name="x_sq")
            dist = apool.tile([P, 2, n], F32, name="dist")
            dist_sq = apool.tile([P, 2, n], F32, name="dist_sq")
            fold = apool.tile([P, n], F32, name="fold")
            half_p = apool.tile([P, n], F32, name="half_p")
            p_sq = apool.tile([P, 2, n], F32, name="p_sq")
            nc.scalar.activation(out=x_sq[:, 0, :], in_=xf, func=ACT.Square, bias=0.2 * SX, scale=SX)
            nc.scalar.activation(out=x_sq[:, 1, :], in_=xf, func=ACT.Square, bias=-0.2 * SX, scale=SX)
            nc.scalar.activation(out=dist[:, 0, :], in_=xf, func=ACT.Abs, bias=-0.5, scale=2.5)
            nc.scalar.activation(out=dist[:, 1, :], in_=xf, func=ACT.Abs, bias=0.5, scale=2.5)
            live[("act", e)] = (x_sq, dist, dist_sq, half_p, p_sq)
            live[("fold", e)] = fold

        def scalar_rest(e):
            x_sq, dist, dist_sq, half_p, p_sq = live[("act", e)]
            fold = live[("fold", e)]
            nc.scalar.activation(out=fold[:], in_=dist[:, 0, :], func=ACT.Abs, bias=-1.0, scale=1.0)
            nc.scalar.activation(out=dist_sq[:], in_=dist[:], func=ACT.Square, bias=-2.0 * K6, scale=K6)
            nc.scalar.activation(out=half_p[:], in_=fold[:], func=ACT.Abs, bias=-0.5, scale=0.5)
            nc.scalar.activation(out=p_sq[:, 0, :], in_=fold[:], func=ACT.Square, bias=-1.0, scale=1.0)
            nc.scalar.activation(out=p_sq[:, 1, :], in_=half_p[:], func=ACT.Square, bias=1.0, scale=-2.0)

        def regroup_g(c):
            for h in range(GH):
                cols = slice(h * OUTS // GH, (h + 1) * OUTS // GH)
                nc.vector.tensor_copy(
                    out=g_grp[:, c, cols, :].rearrange("p (a b) j -> p a j b", b=4),
                    in_=g_raw[:, c, :, cols].rearrange("p j (a b) -> p a j b", b=4),
                )

        def cubes_of(e):
            if ("cubes", e) not in live:
                cubes = vtwo.tile([P, 4, PASSES * SIZES[e] * PACK], BF16, name="cubes")
                live[("cubes", e)] = cubes
            return live[("cubes", e)]

        def vector_first(e):
            n = PASSES * SIZES[e] * PACK
            xf = live[("xf", e)]
            x_sq = live[("act", e)][0]
            cubes = cubes_of(e)
            nc.vector.scalar_tensor_tensor(
                out=cubes[:, 1, :], in0=xf, scalar=0.2, in1=x_sq[:, 0, :], op0=ALU.add, op1=ALU.mult,
            )
            nc.vector.scalar_tensor_tensor(
                out=cubes[:, 2, :], in0=xf, scalar=0.2, in1=x_sq[:, 1, :], op0=ALU.subtract, op1=ALU.mult,
            )

        def far_cubes(e):
            x_sq, dist, dist_sq, half_p, p_sq = live[("act", e)]
            cubes = cubes_of(e)
            if e >= G0:
                nc.vector.scalar_tensor_tensor(
                    out=cubes[:, 0, :], in0=dist[:, 0, :], scalar=2.0, in1=dist_sq[:, 0, :],
                    op0=ALU.subtract, op1=ALU.mult,
                )
            else:
                nc.vector.scalar_tensor_tensor(
                    out=cubes[:, 0:4:3, :], in0=dist[:], scalar=2.0, in1=dist_sq[:],
                    op0=ALU.subtract, op1=ALU.mult,
                )

        def lift_distance(e):
            n = PASSES * SIZES[e] * PACK
            dist = live[("act", e)][1]
            banks = []
            for b in range(n // BANK):
                dp = dpsum.tile([P, BANK], F32, name="dp")
                nc.tensor.matmul(
                    out=dp[:], lhsT=ident32[:], rhs=dist[:, 1, b * BANK : (b + 1) * BANK], start=True, stop=True,
                )
                banks.append(dp)
            live[("dp", e)] = banks

        def far_cube_from_psum(e):
            dist_sq = live[("act", e)][2]
            cubes = cubes_of(e)
            for b, dp in enumerate(live[("dp", e)]):
                cols = slice(b * BANK, (b + 1) * BANK)
                nc.vector.scalar_tensor_tensor(
                    out=cubes[:, 3, cols], in0=dp[:], scalar=2.0, in1=dist_sq[:, 1, cols],
                    op0=ALU.subtract, op1=ALU.mult,
                )

        def hump_products(e):
            n = PASSES * SIZES[e] * PACK
            x_sq, dist, dist_sq, half_p, p_sq = live[("act", e)]
            hump_raw = vone.tile([P, 2, n], F32, name="hump_raw")
            nc.vector.scalar_tensor_tensor(
                out=hump_raw[:, 0, :], in0=half_p[:], scalar=1.0, in1=p_sq[:, 0, :],
                op0=ALU.subtract, op1=ALU.mult,
            )
            nc.vector.scalar_tensor_tensor(
                out=hump_raw[:, 1, :], in0=half_p[:], scalar=0.5, in1=p_sq[:, 1, :],
                op0=ALU.add, op1=ALU.mult,
            )
            live[("hump_raw", e)] = hump_raw

        def round_humps(e):
            n = PASSES * SIZES[e] * PACK
            hump_raw = live[("hump_raw", e)]
            hump = vone.tile([P, 2, n], BF16, name="hump")
            if e >= G0:
                nc.gpsimd.tensor_scalar(
                    out=hump[:, 0, :], in0=hump_raw[:, 1, :], scalar1=-1.0, scalar2=TWO3,
                    op0=ALU.mult, op1=ALU.add,
                )
                if e == nch - 1:
                    nc.scalar.activation(
                        out=hump[:, 1, :], in_=hump_raw[:, 0, :], func=ACT.Identity, bias=TWO3, scale=1.0,
                    )
                else:
                    nc.gpsimd.tensor_scalar(
                        out=hump[:, 1, :], in0=hump_raw[:, 0, :], scalar1=1.0, scalar2=TWO3,
                        op0=ALU.mult, op1=ALU.add,
                    )
            else:
                nc.vector.tensor_scalar(
                    out=hump[:, 1, :], in0=hump_raw[:, 0, :], scalar1=TWO3, scalar2=None, op0=ALU.add,
                )
                nc.vector.tensor_scalar(
                    out=hump[:, 0, :], in0=hump_raw[:, 1, :], scalar1=-1.0, scalar2=TWO3,
                    op0=ALU.mult, op1=ALU.add,
                )
            live[("hump", e)] = hump

        def relu_far_on_scalar(e):
            basis = vtwo.tile([P, PASSES * SIZES[e] // GRP, SPL, M], BF16, name="basis", align_bytes=64)
            live[("basis", e)] = basis
            cubes_v = live[("cubes", e)][:].rearrange("p q (a m) -> p a q m", m=M)
            nc.scalar.activation(out=basis[:, :, 4, :], in_=cubes_v[:, :, 0, :], func=ACT.Relu, bias=0.0, scale=-1.0)
            nc.scalar.activation(out=basis[:, :, 0, :], in_=cubes_v[:, :, 0, :], func=ACT.Relu, bias=0.0, scale=1.0)

        def select(e):
            size = SIZES[e]
            cubes = live[("cubes", e)]
            hump = live[("hump", e)]
            blocks = PASSES * size // GRP
            cubes_v = cubes[:].rearrange("p q (a m) -> p a q m", m=M)
            if e == nch - 1:
                basis = live[("basis", e)]
            else:
                basis = vtwo.tile([P, blocks, SPL, M], BF16, name="basis", align_bytes=64)
                nc.vector.tensor_scalar(
                    out=basis[:, :, 4, :], in0=cubes_v[:, :, 0, :], scalar1=-1.0, scalar2=0.0,
                    op0=ALU.mult, op1=ALU.max,
                )
                nc.vector.tensor_scalar(
                    out=basis[:, :, 0, :], in0=cubes_v[:, :, 0, :], scalar1=0.0, scalar2=None, op0=ALU.max,
                )
            nc.vector.tensor_scalar(
                out=basis[:, :, 1:4, :], in0=cubes_v[:, :, 1:4, :], scalar1=-1.0, scalar2=0.0,
                op0=ALU.mult, op1=ALU.max,
            )
            nc.vector.tensor_scalar(
                out=basis[:, :, 5:8, :], in0=cubes_v[:, :, 1:4, :], scalar1=0.0, scalar2=None, op0=ALU.max,
            )
            hump_v = hump[:].rearrange("p r (a m) -> p a r m", m=M)
            live[("basis", e)] = basis
            if e < nch - 1:
                for l in (1, 3, 5):
                    nc.vector.tensor_tensor(
                        out=basis[:, :, l : l + 2, :], in0=basis[:, :, l : l + 2, :], in1=hump_v, op=ALU.min,
                    )
                return

            def clamp(c, l):
                nc.vector.tensor_tensor(
                    out=basis[:, c, l : l + 2, :], in0=basis[:, c, l : l + 2, :], in1=hump_v[:, c], op=ALU.min,
                )

            b_codes = cpool.tile([P, PASSES, W], U32, name="b_codes", align_bytes=64)
            b_scales = cpool.tile([P, PASSES, W], U8, name="b_scales", align_bytes=64)
            live[("codes", e)] = (b_codes, b_scales)

            def pack(c, l0, l1):
                nc.vector.quantize_mx(
                    out=b_codes[:, c, l0 * GRP : l1 * GRP].bitcast(E4),
                    scales=b_scales[:, c, l0 * GRP : l1 * GRP],
                    in_=basis[:, c, l0:l1, :].rearrange("p l m -> p (l m)"),
                )

            clamp(0, 1)
            clamp(0, 3)
            clamp(0, 5)
            clamp(1, 1)
            clamp(1, 3)
            pack(0, 0, SPL)
            clamp(1, 5)
            pack(1, 0, SPL // 2)
            pack(1, SPL // 2, SPL)

        def quantise(e):
            size = SIZES[e]
            basis = live[("basis", e)]
            per = size // GRP
            b_codes = cpool.tile([P, PASSES, size * SPL], U32, name="b_codes", align_bytes=64)
            b_scales = cpool.tile([P, PASSES, size * SPL], U8, name="b_scales", align_bytes=64)
            if size > GRP:
                for c in range(PASSES):
                    nc.vector.quantize_mx(
                        out=b_codes[:, c, :].bitcast(E4),
                        scales=b_scales[:, c, :],
                        in_=basis[:, c * per : (c + 1) * per].rearrange("p k l m -> p (k l m)"),
                    )
            else:
                nc.vector.quantize_mx(
                    out=b_codes[:].rearrange("p c w -> p (c w)").bitcast(E4),
                    scales=b_scales[:].rearrange("p c w -> p (c w)"),
                    in_=basis[:].rearrange("p a l m -> p (a l m)"),
                )
            live[("codes", e)] = (b_codes, b_scales)

        def multiply(e, k):
            b_codes, b_scales = live[("codes", e)]
            banks = [psum.tile([P, W], F32, name="acc") for t in range(OT)]
            if e == nch - 1:
                order = [(c, t) for c in range(PASSES) for t in range(OT)]
            else:
                order = [(c, t) for t in range(OT) for c in range(PASSES)]
            for c, t in order:
                nc.tensor.matmul_mx(
                    out=banks[t][:],
                    lhsT=g_codes[:, c, t * P : (t + 1) * P].bitcast(E5),
                    lhsT_scale=g_scales[:, c, t * P : (t + 1) * P],
                    rhs=b_codes[:, c, k * W : (k + 1) * W].bitcast(E4),
                    rhs_scale=b_scales[:, c, k * W : (k + 1) * W],
                    start=(c == 0),
                    stop=(c == PASSES - 1),
                )
            live[("banks", e, k)] = banks

        def empty(e, k, last):
            banks = live[("banks", e, k)]
            res = stage.tile([P, OT, W], F32, name="res")
            first_col = (starts[e] + k * GRP) * SPL
            cols = slice(first_col, first_col + W)
            for t in range(OT):
                if last and t % 2 == 1:
                    nc.vector.tensor_copy(
                        out=res[:, t, :].rearrange("p (i l) -> p i l", l=SPL),
                        in_=banks[t][:].rearrange("p (l i) -> p i l", l=SPL),
                    )
                else:
                    nc.scalar.copy(
                        out=res[:, t, :].rearrange("p (i l) -> p i l", l=SPL),
                        in_=banks[t][:].rearrange("p (l i) -> p i l", l=SPL),
                    )
                if last:
                    nc.sync.dma_start(out=out_v[:, t, cols], in_=res[:, t, :])
            if not last:
                nc.sync.dma_start(out=out_v[:, :, cols], in_=res[:])

        regroup(0)
        regroup(1)
        scalar_reads(0)
        scalar_rest(0)
        scalar_reads(1)
        scalar_rest(1)
        regroup_g(0)
        regroup_g(1)
        vector_first(0)
        nc.vector.quantize_mx(
            out=g_codes[:].rearrange("p c o -> p (c o)").bitcast(E5),
            scales=g_scales[:].rearrange("p c o -> p (c o)"),
            in_=g_grp[:].rearrange("p c o j -> p (c o j)"),
        )
        far_cubes(0)
        hump_products(0)
        round_humps(0)
        for e in range(nch):
            if e >= G0:
                vector_first(e)
                far_cube_from_psum(e)
            if e + 2 < nch:
                regroup(e + 2)
            if e + 1 >= G0 and e + 1 < nch:
                lift_distance(e + 1)
            select(e)
            if e + 1 < G0:
                vector_first(e + 1)
            if e + 1 >= G0 and e + 1 < nch:
                far_cubes(e + 1)
            if e + 1 == nch - 1:
                relu_far_on_scalar(e + 1)
            if e < nch - 1:
                quantise(e)
            if e + 1 < G0:
                far_cubes(e + 1)
            if e + 1 < nch:
                hump_products(e + 1)
                round_humps(e + 1)
            if e + 2 < nch:
                scalar_reads(e + 2)
                scalar_rest(e + 2)
            for k in range(SIZES[e] // GRP):
                multiply(e, k)
                empty(e, k, e == nch - 1)
